import numpy as np
import ml_dtypes

BF16 = ml_dtypes.bfloat16


def bf(x):
    return np.asarray(x, np.float32).astype(BF16)


def f32(x):
    return np.asarray(x, np.float32)


def f64(x):
    return np.asarray(x).astype(np.float64)


def striped(idx):
    return np.tile(idx.reshape(-1, 16).T, (8, 1))


C, V, T, B, HEADS, HEAD, N = 512, 1024, 512, 4, 4, 128, 2048
EPS = 1e-5
AQ, AK, AV, AO = 0.09375, 0.0625, 0.0625, 0.125


def ternary(a):
    z = np.random.standard_normal((C, C))
    return bf(a * np.sign(z) * (np.abs(z) > 0.7 * np.mean(np.abs(z))))


def column(mean):
    return f32(mean + 0.1 * np.random.standard_normal((C, 1)))


def layer_norm(a, gain, shift):
    mu = a.mean(axis=0, keepdims=True)
    var = ((a - mu) ** 2).mean(axis=0, keepdims=True)
    return (a - mu) / np.sqrt(var + EPS) * gain + shift


def setup_inputs():
    return {"tok": f32(np.random.standard_normal((C, V))), "pos": f32(np.random.standard_normal((C, T))), "gain0": column(1.0), "shift0": column(0.0), "wq": ternary(AQ), "bq": column(0.0), "wk": ternary(AK), "wv": ternary(AV), "bv": column(0.0), "wo": ternary(AO), "bo": column(0.0), "gain1": column(1.0), "shift1": column(0.0), "offs": striped(np.concatenate([np.random.permutation(V)[:T] for _ in range(B)]))}


def reference(tok, pos, gain0, shift0, wq, bq, wk, wv, bv, wo, bo, gain1, shift1, offs):
    idx = offs[:16].T.reshape(-1)
    x = f64(tok)[:, idx] + np.tile(f64(pos), (1, B))
    y = layer_norm(x, f64(gain0), f64(shift0))
    q = (f64(wq).T @ y + f64(bq)).reshape(HEADS, HEAD, B, T)
    k = (f64(wk).T @ y).reshape(HEADS, HEAD, B, T)
    v = (f64(wv).T @ y + f64(bv)).reshape(HEADS, HEAD, B, T)
    s = (q.transpose(0, 2, 3, 1) @ k.transpose(0, 2, 1, 3)) / np.sqrt(HEAD)
    p = np.exp(s - s.max(axis=-1, keepdims=True))
    p = p / p.sum(axis=-1, keepdims=True)
    ctx = (v.transpose(0, 2, 1, 3) @ p.transpose(0, 1, 3, 2)).transpose(0, 2, 1, 3).reshape(C, N)
    z = y + f64(wo).T @ ctx + f64(bo)
    return layer_norm(z, f64(gain1), f64(shift1))

@@ -1,0 +1,233 @@
+from contextlib import ExitStack
+
+import concourse.mybir as mybir
+from concourse.masks import make_identity
+
+F32, BF16, U16 = mybir.dt.float32, mybir.dt.bfloat16, mybir.dt.uint16
+ALU = mybir.AluOpType
+FUNC = mybir.ActivationFunctionType
+FREE_AXIS = mybir.AxisListType.X
+
+P = 128
+C = 512
+WORDS = 1024
+T = 512
+SEQS = 4
+N = SEQS * T
+CB = C // P
+TB = T // P
+EPS = 1e-5
+SCORE_SCALE = P**-0.5
+GAIN0, SHIFT0, BQ, BO, GAIN1, SHIFT1 = 0, 1, 2, 3, 4, 5
+
+FLOPS = 4 * 2 * C * C * N + 2 * 2 * SEQS * CB * T * T * P
+
+
+def block(i):
+    return slice(i * P, (i + 1) * P)
+
+
+def tile_ternaryberttiny_b_kernel(
+    tc, tok, pos, gain0, shift0, wq, bq, wk, wv, bv, wo, bo, gain1, shift1, offs, out
+):
+    nc = tc.nc
+    with ExitStack() as pools:
+        held = pools.enter_context(tc.tile_pool(name="held", bufs=1))
+        seq = pools.enter_context(tc.tile_pool(name="seq", bufs=2))
+        work = pools.enter_context(tc.tile_pool(name="work", bufs=3))
+        small = pools.enter_context(tc.tile_pool(name="small", bufs=4))
+        acc = pools.enter_context(tc.psum_pool(name="acc", bufs=4))
+        score = pools.enter_context(tc.psum_pool(name="score", bufs=2))
+        flip = pools.enter_context(tc.psum_pool(name="flip", bufs=2))
+
+        offsets = held.tile([P, N // 16], U16, name="offsets")
+        nc.sync.dma_start(offsets[:], offs)
+        tok_sb = [held.tile([P, WORDS], F32, name=f"tok{cb}") for cb in range(CB)]
+        pos_sb = [held.tile([P, T], F32, name=f"pos{cb}") for cb in range(CB)]
+        for cb in range(CB):
+            nc.sync.dma_start(tok_sb[cb][:], tok[block(cb), :])
+            nc.scalar.dma_start(pos_sb[cb][:], pos[block(cb), :])
+
+        rows = held.tile([P, C], F32, name="rows")
+        nc.vector.memset(rows[:], 0.0)
+        for k, vector in enumerate((gain0, shift0, bq, bo, gain1, shift1)):
+            nc.scalar.dma_start(rows[k : k + 1, :], vector.rearrange("c one -> one c"))
+        weights = {}
+        for name, w in (("q", wq), ("k", wk), ("v", wv), ("o", wo)):
+            weights[name] = held.tile([P, CB, C], BF16, name=f"w{name}")
+            nc.sync.dma_start(weights[name][:], w.rearrange("(cb p) m -> p cb m", p=P))
+        bv_rows = held.tile([P, C], F32, name="bv_rows")
+        nc.scalar.dma_start(bv_rows[:], bv.rearrange("c one -> (c one)").partition_broadcast(P))
+
+        ident_f32 = held.tile([P, P], F32, name="ident_f32")
+        make_identity(nc, ident_f32[:])
+        ident_bf16 = held.tile([P, P], BF16, name="ident_bf16")
+        make_identity(nc, ident_bf16[:])
+        minus_half = held.tile([P, 1], F32, name="minus_half")
+        nc.vector.memset(minus_half[:], -0.5)
+
+        cols_ps = acc.tile([P, C], F32, name="cols_ps", tag="acc")
+        for cb in range(CB):
+            nc.tensor.transpose(cols_ps[:, block(cb)], rows[:, block(cb)], ident_f32[:])
+        cols = held.tile([P, C], F32, name="cols")
+        nc.vector.tensor_copy(cols[:], cols_ps[:])
+
+        def column(k, cb):
+            return cols[:, cb * P + k : cb * P + k + 1]
+
+        def standardise(a, name):
+            flipped = []
+            for tb in range(TB):
+                a_ps = acc.tile([P, C], F32, name="a_ps", tag="acc")
+                for cb in range(CB):
+                    nc.tensor.transpose(a_ps[:, block(cb)], a[cb][:, block(tb)], ident_f32[:])
+                stats = small.tile([P, 6], F32, name="stats")
+                nc.vector.bn_stats(stats[:], a_ps[:])
+                mean_var = small.tile([P, 2], F32, name="mean_var")
+                nc.vector.bn_aggr(mean_var[:], stats[:])
+                var_eps = small.tile([P, 1], F32, name="var_eps")
+                nc.vector.tensor_scalar_add(var_eps[:], mean_var[:, 1:2], EPS)
+                rstd = small.tile([P, 1], F32, name="rstd")
+                nc.gpsimd.tensor_tensor(rstd[:], var_eps[:], minus_half[:], ALU.pow)
+                minus_mean_rstd = small.tile([P, 1], F32, name="minus_mean_rstd")
+                nc.vector.scalar_tensor_tensor(
+                    minus_mean_rstd[:], mean_var[:, 0:1], -1.0, rstd[:], ALU.mult, ALU.mult
+                )
+                a_hat = seq.tile([P, C], F32, name=f"{name}{tb}")
+                nc.scalar.activation(
+                    a_hat[:], a_ps[:], FUNC.Identity, bias=minus_mean_rstd[:], scale=rstd[:]
+                )
+                flipped.append(a_hat)
+            return flipped
+
+        def channels_first(flipped, cb):
+            back_ps = acc.tile([P, T], F32, name="back_ps", tag="acc")
+            for tb in range(TB):
+                nc.tensor.transpose(back_ps[:, block(tb)], flipped[tb][:, block(cb)], ident_f32[:])
+            return back_ps
+
+        def embed(r):
+            x = []
+            for cb in range(CB):
+                x_cb = seq.tile([P, T], F32, name=f"x{cb}")
+                piece = offsets[:, r * (T // 16) : (r + 1) * (T // 16)]
+                nc.vector.tensor_tensor(
+                    x_cb[:], tok_sb[cb][:].indirect(piece), pos_sb[cb][:], ALU.add
+                )
+                x.append(x_cb)
+            x_hat = standardise(x, "x_hat")
+            y, y_bf = [], []
+            for cb in range(CB):
+                back_ps = channels_first(x_hat, cb)
+                y_cb = seq.tile([P, T], F32, name=f"y{cb}")
+                nc.scalar.activation(
+                    y_cb[:], back_ps[:], FUNC.Identity,
+                    bias=column(SHIFT0, cb), scale=column(GAIN0, cb),
+                )
+                y_bf_cb = seq.tile([P, T], BF16, name=f"y_bf{cb}")
+                nc.gpsimd.tensor_copy(y_bf_cb[:], y_cb[:])
+                y.append(y_cb)
+                y_bf.append(y_bf_cb)
+            return y, y_bf
+
+        def project(y_bf):
+            q, k, v = [], [], []
+            for mb in range(CB):
+                q_ps = acc.tile([P, T], F32, name="q_ps", tag="acc")
+                for cb in range(CB):
+                    nc.tensor.matmul(
+                        q_ps[:], weights["q"][:, cb, block(mb)], y_bf[cb][:],
+                        start=cb == 0, stop=cb == CB - 1,
+                    )
+                q_mb = seq.tile([P, T], BF16, name=f"q{mb}")
+                nc.scalar.activation(q_mb[:], q_ps[:], FUNC.Identity, bias=column(BQ, mb))
+                q.append(q_mb)
+                k_ps = acc.tile([P, T], F32, name="k_ps", tag="acc")
+                for cb in range(CB):
+                    nc.tensor.matmul(
+                        k_ps[:], weights["k"][:, cb, block(mb)], y_bf[cb][:],
+                        start=cb == 0, stop=cb == CB - 1,
+                    )
+                k_mb = seq.tile([P, T], BF16, name=f"k{mb}")
+                nc.scalar.copy(k_mb[:], k_ps[:])
+                k.append(k_mb)
+            for tb in range(TB):
+                v_ps = acc.tile([P, C], F32, name="v_ps", tag="acc")
+                for cb in range(CB):
+                    nc.tensor.matmul(
+                        v_ps[:], y_bf[cb][:, block(tb)], weights["v"][:, cb, :],
+                        start=cb == 0, stop=cb == CB - 1,
+                    )
+                v_tb = seq.tile([P, C], BF16, name=f"v{tb}")
+                nc.vector.tensor_tensor(v_tb[:], v_ps[:], bv_rows[:], ALU.add)
+                v.append(v_tb)
+            return q, k, v
+
+        def attend(q, k, v):
+            ctx = []
+            for h in range(CB):
+                p_flipped = work.tile([P, TB, T], BF16, name="p_flipped")
+                for tb in range(TB):
+                    s_ps = score.tile([P, T], F32, name="s_ps")
+                    nc.tensor.matmul(s_ps[:], q[h][:, block(tb)], k[h][:], start=True, stop=True)
+                    minus_max = small.tile([P, 1], F32, name="minus_max")
+                    nc.vector.reduce_max(minus_max[:], s_ps[:], axis=FREE_AXIS, negate=True)
+                    exp_bias = small.tile([P, 1], F32, name="exp_bias")
+                    nc.scalar.mul(exp_bias[:], minus_max[:], SCORE_SCALE)
+                    e = work.tile([P, T], F32, name="e")
+                    e_sum = small.tile([P, 1], F32, name="e_sum")
+                    nc.scalar.activation(
+                        e[:], s_ps[:], FUNC.Exp, bias=exp_bias[:], scale=SCORE_SCALE,
+                        accum_out=e_sum[:],
+                    )
+                    one_over_sum = small.tile([P, 1], F32, name="one_over_sum")
+                    nc.vector.reciprocal(one_over_sum[:], e_sum[:])
+                    p = work.tile([P, T], BF16, name="p")
+                    nc.gpsimd.tensor_scalar(p[:], e[:], one_over_sum[:], 1.0, ALU.mult, ALU.mult)
+                    p_ps = flip.tile([P, TB, P], BF16, name="p_ps")
+                    for ub in range(TB):
+                        nc.tensor.transpose(p_ps[:, ub, :], p[:, block(ub)], ident_bf16[:])
+                    nc.vector.tensor_copy(p_flipped[:, :, block(tb)], p_ps[:])
+                ctx_ps = acc.tile([P, T], F32, name="ctx_ps", tag="acc")
+                for ub in range(TB):
+                    nc.tensor.matmul(
+                        ctx_ps[:], v[ub][:, block(h)], p_flipped[:, ub, :],
+                        start=ub == 0, stop=ub == TB - 1,
+                    )
+                ctx_h = seq.tile([P, T], BF16, name=f"ctx{h}")
+                nc.scalar.copy(ctx_h[:], ctx_ps[:])
+                ctx.append(ctx_h)
+            return ctx
+
+        def finish(r, y, ctx):
+            z = []
+            for mb in range(CB):
+                o_ps = acc.tile([P, T], F32, name="o_ps", tag="acc")
+                for cb in range(CB):
+                    nc.tensor.matmul(
+                        o_ps[:], weights["o"][:, cb, block(mb)], ctx[cb][:],
+                        start=cb == 0, stop=cb == CB - 1,
+                    )
+                z_mb = seq.tile([P, T], F32, name=f"z{mb}")
+                nc.vector.scalar_tensor_tensor(
+                    z_mb[:], o_ps[:], column(BO, mb), y[mb][:], ALU.add, ALU.add
+                )
+                z.append(z_mb)
+            z_hat = standardise(z, "z_hat")
+            for cb in range(CB):
+                back_ps = channels_first(z_hat, cb)
+                out_cb = work.tile([P, T], F32, name="out_cb")
+                nc.scalar.activation(
+                    out_cb[:], back_ps[:], FUNC.Identity,
+                    bias=column(SHIFT1, cb), scale=column(GAIN1, cb),
+                )
+                nc.sync.dma_start(out[block(cb), r * T : (r + 1) * T], out_cb[:])
+
+        embedded = embed(0)
+        for r in range(SEQS):
+            y, y_bf = embedded
+            q, k, v = project(y_bf)
+            if r + 1 < SEQS:
+                embedded = embed(r + 1)
+            ctx = attend(q, k, v)
+            finish(r, y, ctx)

@@ -6,7 +6,6 @@ from concourse.masks import make_identity
 F32, BF16, U16 = mybir.dt.float32, mybir.dt.bfloat16, mybir.dt.uint16
 ALU = mybir.AluOpType
 FUNC = mybir.ActivationFunctionType
-FREE_AXIS = mybir.AxisListType.X
 
 P = 128
 C = 512
@@ -33,12 +32,14 @@ def tile_ternaryberttiny_b_kernel(
     nc = tc.nc
     with ExitStack() as pools:
         held = pools.enter_context(tc.tile_pool(name="held", bufs=1))
-        seq = pools.enter_context(tc.tile_pool(name="seq", bufs=2))
-        work = pools.enter_context(tc.tile_pool(name="work", bufs=3))
-        small = pools.enter_context(tc.tile_pool(name="small", bufs=4))
-        acc = pools.enter_context(tc.psum_pool(name="acc", bufs=4))
+        once = pools.enter_context(tc.tile_pool(name="once", bufs=1))
+        twice = pools.enter_context(tc.tile_pool(name="twice", bufs=2))
+        thrice = pools.enter_context(tc.tile_pool(name="thrice", bufs=3))
+        ring = pools.enter_context(tc.tile_pool(name="ring", bufs=4))
+        flip_ln = pools.enter_context(tc.psum_pool(name="flip_ln", bufs=2))
+        product = pools.enter_context(tc.psum_pool(name="product", bufs=2))
         score = pools.enter_context(tc.psum_pool(name="score", bufs=2))
-        flip = pools.enter_context(tc.psum_pool(name="flip", bufs=2))
+        flip_p = pools.enter_context(tc.psum_pool(name="flip_p", bufs=2))
 
         offsets = held.tile([P, N // 16], U16, name="offsets")
         nc.sync.dma_start(offsets[:], offs)
@@ -52,12 +53,12 @@ def tile_ternaryberttiny_b_kernel(
         nc.vector.memset(rows[:], 0.0)
         for k, vector in enumerate((gain0, shift0, bq, bo, gain1, shift1)):
             nc.scalar.dma_start(rows[k : k + 1, :], vector.rearrange("c one -> one c"))
-        weights = {}
-        for name, w in (("q", wq), ("k", wk), ("v", wv), ("o", wo)):
-            weights[name] = held.tile([P, CB, C], BF16, name=f"w{name}")
-            nc.sync.dma_start(weights[name][:], w.rearrange("(cb p) m -> p cb m", p=P))
         bv_rows = held.tile([P, C], F32, name="bv_rows")
         nc.scalar.dma_start(bv_rows[:], bv.rearrange("c one -> (c one)").partition_broadcast(P))
+        weights = {}
+        for name, w in (("v", wv), ("q", wq), ("k", wk), ("o", wo)):
+            weights[name] = held.tile([P, CB, C], BF16, name=f"w{name}")
+            nc.sync.dma_start(weights[name][:], w.rearrange("(cb p) m -> p cb m", p=P))
 
         ident_f32 = held.tile([P, P], F32, name="ident_f32")
         make_identity(nc, ident_f32[:])
@@ -66,7 +67,7 @@ def tile_ternaryberttiny_b_kernel(
         minus_half = held.tile([P, 1], F32, name="minus_half")
         nc.vector.memset(minus_half[:], -0.5)
 
-        cols_ps = acc.tile([P, C], F32, name="cols_ps", tag="acc")
+        cols_ps = product.tile([P, C], F32, name="cols_ps", tag="product")
         for cb in range(CB):
             nc.tensor.transpose(cols_ps[:, block(cb)], rows[:, block(cb)], ident_f32[:])
         cols = held.tile([P, C], F32, name="cols")
@@ -75,159 +76,183 @@ def tile_ternaryberttiny_b_kernel(
         def column(k, cb):
             return cols[:, cb * P + k : cb * P + k + 1]
 
+        x, x_hat, y, y_bf = {}, {}, {}, {}
+        q, k, v, p_flipped, ctx = {}, {}, {}, {}, {}
+        z, z_hat = {}, {}
+
         def standardise(a, name):
             flipped = []
             for tb in range(TB):
-                a_ps = acc.tile([P, C], F32, name="a_ps", tag="acc")
+                a_ps = flip_ln.tile([P, C], F32, name="a_ps")
                 for cb in range(CB):
                     nc.tensor.transpose(a_ps[:, block(cb)], a[cb][:, block(tb)], ident_f32[:])
-                stats = small.tile([P, 6], F32, name="stats")
-                nc.vector.bn_stats(stats[:], a_ps[:])
-                mean_var = small.tile([P, 2], F32, name="mean_var")
+                a_sb = ring.tile([P, C], F32, name="a_sb")
+                nc.scalar.copy(a_sb[:], a_ps[:])
+                stats = ring.tile([P, 6], F32, name="stats")
+                nc.vector.bn_stats(stats[:], a_sb[:])
+                mean_var = ring.tile([P, 2], F32, name="mean_var")
                 nc.vector.bn_aggr(mean_var[:], stats[:])
-                var_eps = small.tile([P, 1], F32, name="var_eps")
+                var_eps = ring.tile([P, 1], F32, name="var_eps")
                 nc.vector.tensor_scalar_add(var_eps[:], mean_var[:, 1:2], EPS)
-                rstd = small.tile([P, 1], F32, name="rstd")
+                rstd = ring.tile([P, 1], F32, name="rstd")
                 nc.gpsimd.tensor_tensor(rstd[:], var_eps[:], minus_half[:], ALU.pow)
-                minus_mean_rstd = small.tile([P, 1], F32, name="minus_mean_rstd")
-                nc.vector.scalar_tensor_tensor(
-                    minus_mean_rstd[:], mean_var[:, 0:1], -1.0, rstd[:], ALU.mult, ALU.mult
-                )
-                a_hat = seq.tile([P, C], F32, name=f"{name}{tb}")
-                nc.scalar.activation(
-                    a_hat[:], a_ps[:], FUNC.Identity, bias=minus_mean_rstd[:], scale=rstd[:]
+                a_hat = once.tile([P, C], F32, name=f"{name}{tb}")
+                nc.vector.tensor_scalar(
+                    a_hat[:], a_sb[:], mean_var[:, 0:1], rstd[:], ALU.subtract, ALU.mult
                 )
                 flipped.append(a_hat)
             return flipped
 
         def channels_first(flipped, cb):
-            back_ps = acc.tile([P, T], F32, name="back_ps", tag="acc")
+            back_ps = product.tile([P, T], F32, name="back_ps", tag="product")
             for tb in range(TB):
                 nc.tensor.transpose(back_ps[:, block(tb)], flipped[tb][:, block(cb)], ident_f32[:])
             return back_ps
 
-        def embed(r):
-            x = []
+        def gather(r):
+            piece = offsets[:, r * (T // 16) : (r + 1) * (T // 16)]
+            x[r] = []
             for cb in range(CB):
-                x_cb = seq.tile([P, T], F32, name=f"x{cb}")
-                piece = offsets[:, r * (T // 16) : (r + 1) * (T // 16)]
+                x_cb = twice.tile([P, T], F32, name=f"x{cb}")
                 nc.vector.tensor_tensor(
                     x_cb[:], tok_sb[cb][:].indirect(piece), pos_sb[cb][:], ALU.add
                 )
-                x.append(x_cb)
-            x_hat = standardise(x, "x_hat")
-            y, y_bf = [], []
+                x[r].append(x_cb)
+
+        def standardise_x(r):
+            x_hat[r] = standardise(x[r], "x_hat")
+
+        def make_y(r):
+            y[r], y_bf[r] = [], []
             for cb in range(CB):
-                back_ps = channels_first(x_hat, cb)
-                y_cb = seq.tile([P, T], F32, name=f"y{cb}")
+                back_ps = channels_first(x_hat[r], cb)
+                y_cb = thrice.tile([P, T], F32, name=f"y{cb}")
                 nc.scalar.activation(
                     y_cb[:], back_ps[:], FUNC.Identity,
                     bias=column(SHIFT0, cb), scale=column(GAIN0, cb),
                 )
-                y_bf_cb = seq.tile([P, T], BF16, name=f"y_bf{cb}")
+                y_bf_cb = twice.tile([P, T], BF16, name=f"y_bf{cb}")
                 nc.gpsimd.tensor_copy(y_bf_cb[:], y_cb[:])
-                y.append(y_cb)
-                y_bf.append(y_bf_cb)
-            return y, y_bf
+                y[r].append(y_cb)
+                y_bf[r].append(y_bf_cb)
 
-        def project(y_bf):
-            q, k, v = [], [], []
-            for mb in range(CB):
-                q_ps = acc.tile([P, T], F32, name="q_ps", tag="acc")
-                for cb in range(CB):
-                    nc.tensor.matmul(
-                        q_ps[:], weights["q"][:, cb, block(mb)], y_bf[cb][:],
-                        start=cb == 0, stop=cb == CB - 1,
-                    )
-                q_mb = seq.tile([P, T], BF16, name=f"q{mb}")
-                nc.scalar.activation(q_mb[:], q_ps[:], FUNC.Identity, bias=column(BQ, mb))
-                q.append(q_mb)
-                k_ps = acc.tile([P, T], F32, name="k_ps", tag="acc")
-                for cb in range(CB):
-                    nc.tensor.matmul(
-                        k_ps[:], weights["k"][:, cb, block(mb)], y_bf[cb][:],
-                        start=cb == 0, stop=cb == CB - 1,
-                    )
-                k_mb = seq.tile([P, T], BF16, name=f"k{mb}")
-                nc.scalar.copy(k_mb[:], k_ps[:])
-                k.append(k_mb)
+        def project_v(r):
+            v[r] = []
             for tb in range(TB):
-                v_ps = acc.tile([P, C], F32, name="v_ps", tag="acc")
+                v_ps = product.tile([P, C], F32, name="v_ps", tag="product")
                 for cb in range(CB):
                     nc.tensor.matmul(
-                        v_ps[:], y_bf[cb][:, block(tb)], weights["v"][:, cb, :],
+                        v_ps[:], y_bf[r][cb][:, block(tb)], weights["v"][:, cb, :],
                         start=cb == 0, stop=cb == CB - 1,
                     )
-                v_tb = seq.tile([P, C], BF16, name=f"v{tb}")
+                v_tb = twice.tile([P, C], BF16, name=f"v{tb}")
                 nc.vector.tensor_tensor(v_tb[:], v_ps[:], bv_rows[:], ALU.add)
-                v.append(v_tb)
-            return q, k, v
+                v[r].append(v_tb)
 
-        def attend(q, k, v):
-            ctx = []
-            for h in range(CB):
-                p_flipped = work.tile([P, TB, T], BF16, name="p_flipped")
-                for tb in range(TB):
-                    s_ps = score.tile([P, T], F32, name="s_ps")
-                    nc.tensor.matmul(s_ps[:], q[h][:, block(tb)], k[h][:], start=True, stop=True)
-                    minus_max = small.tile([P, 1], F32, name="minus_max")
-                    nc.vector.reduce_max(minus_max[:], s_ps[:], axis=FREE_AXIS, negate=True)
-                    exp_bias = small.tile([P, 1], F32, name="exp_bias")
-                    nc.scalar.mul(exp_bias[:], minus_max[:], SCORE_SCALE)
-                    e = work.tile([P, T], F32, name="e")
-                    e_sum = small.tile([P, 1], F32, name="e_sum")
-                    nc.scalar.activation(
-                        e[:], s_ps[:], FUNC.Exp, bias=exp_bias[:], scale=SCORE_SCALE,
-                        accum_out=e_sum[:],
-                    )
-                    one_over_sum = small.tile([P, 1], F32, name="one_over_sum")
-                    nc.vector.reciprocal(one_over_sum[:], e_sum[:])
-                    p = work.tile([P, T], BF16, name="p")
-                    nc.gpsimd.tensor_scalar(p[:], e[:], one_over_sum[:], 1.0, ALU.mult, ALU.mult)
-                    p_ps = flip.tile([P, TB, P], BF16, name="p_ps")
-                    for ub in range(TB):
-                        nc.tensor.transpose(p_ps[:, ub, :], p[:, block(ub)], ident_bf16[:])
-                    nc.vector.tensor_copy(p_flipped[:, :, block(tb)], p_ps[:])
-                ctx_ps = acc.tile([P, T], F32, name="ctx_ps", tag="acc")
+        def project_qk(r, h):
+            q_ps = product.tile([P, T], F32, name="q_ps", tag="product")
+            for cb in range(CB):
+                nc.tensor.matmul(
+                    q_ps[:], weights["q"][:, cb, block(h)], y_bf[r][cb][:],
+                    start=cb == 0, stop=cb == CB - 1,
+                )
+            q[r, h] = twice.tile([P, T], BF16, name=f"q{h}")
+            nc.scalar.activation(q[r, h][:], q_ps[:], FUNC.Identity, bias=column(BQ, h))
+            k_ps = product.tile([P, T], F32, name="k_ps", tag="product")
+            for cb in range(CB):
+                nc.tensor.matmul(
+                    k_ps[:], weights["k"][:, cb, block(h)], y_bf[r][cb][:],
+                    start=cb == 0, stop=cb == CB - 1,
+                )
+            k[r, h] = twice.tile([P, T], BF16, name=f"k{h}")
+            nc.scalar.copy(k[r, h][:], k_ps[:])
+
+        def probabilities(r, h):
+            p_flipped[r, h] = thrice.tile([P, TB, T], BF16, name="p_flipped")
+            for tb in range(TB):
+                s_ps = score.tile([P, T], F32, name="s_ps")
+                nc.tensor.matmul(
+                    s_ps[:], q[r, h][:, block(tb)], k[r, h][:], start=True, stop=True
+                )
+                minus_s = ring.tile([P, T], F32, name="minus_s")
+                minus_max = ring.tile([P, 1], F32, name="minus_max")
+                nc.vector.tensor_scalar(
+                    minus_s[:], s_ps[:], -SCORE_SCALE, None, ALU.mult, ALU.min,
+                    accum_out=minus_max[:],
+                )
+                e = ring.tile([P, T], F32, name="e")
+                e_sum = ring.tile([P, 1], F32, name="e_sum")
+                nc.scalar.activation(
+                    e[:], minus_s[:], FUNC.Exp, bias=minus_max[:], scale=-1.0, accum_out=e_sum[:]
+                )
+                one_over_sum = ring.tile([P, 1], F32, name="one_over_sum")
+                nc.vector.reciprocal(one_over_sum[:], e_sum[:])
+                p = ring.tile([P, T], BF16, name="p")
+                nc.gpsimd.tensor_scalar(p[:], e[:], one_over_sum[:], 1.0, ALU.mult, ALU.mult)
+                p_ps = flip_p.tile([P, TB, P], BF16, name="p_ps")
                 for ub in range(TB):
-                    nc.tensor.matmul(
-                        ctx_ps[:], v[ub][:, block(h)], p_flipped[:, ub, :],
-                        start=ub == 0, stop=ub == TB - 1,
-                    )
-                ctx_h = seq.tile([P, T], BF16, name=f"ctx{h}")
-                nc.scalar.copy(ctx_h[:], ctx_ps[:])
-                ctx.append(ctx_h)
-            return ctx
+                    nc.tensor.transpose(p_ps[:, ub, :], p[:, block(ub)], ident_bf16[:])
+                nc.vector.tensor_copy(p_flipped[r, h][:, :, block(tb)], p_ps[:])
 
-        def finish(r, y, ctx):
-            z = []
+        def context(r, h):
+            ctx_ps = product.tile([P, T], F32, name="ctx_ps", tag="product")
+            for ub in range(TB):
+                nc.tensor.matmul(
+                    ctx_ps[:], v[r][ub][:, block(h)], p_flipped[r, h][:, ub, :],
+                    start=ub == 0, stop=ub == TB - 1,
+                )
+            ctx[r, h] = twice.tile([P, T], BF16, name=f"ctx{h}")
+            nc.scalar.copy(ctx[r, h][:], ctx_ps[:])
+
+        def project_out(r):
+            z[r] = []
             for mb in range(CB):
-                o_ps = acc.tile([P, T], F32, name="o_ps", tag="acc")
+                o_ps = product.tile([P, T], F32, name="o_ps", tag="product")
                 for cb in range(CB):
                     nc.tensor.matmul(
-                        o_ps[:], weights["o"][:, cb, block(mb)], ctx[cb][:],
+                        o_ps[:], weights["o"][:, cb, block(mb)], ctx[r, cb][:],
                         start=cb == 0, stop=cb == CB - 1,
                     )
-                z_mb = seq.tile([P, T], F32, name=f"z{mb}")
+                z_mb = once.tile([P, T], F32, name=f"z{mb}")
                 nc.vector.scalar_tensor_tensor(
-                    z_mb[:], o_ps[:], column(BO, mb), y[mb][:], ALU.add, ALU.add
+                    z_mb[:], o_ps[:], column(BO, mb), y[r][mb][:], ALU.add, ALU.add
                 )
-                z.append(z_mb)
-            z_hat = standardise(z, "z_hat")
+                z[r].append(z_mb)
+
+        def standardise_z(r):
+            z_hat[r] = standardise(z[r], "z_hat")
+
+        def write_out(r):
             for cb in range(CB):
-                back_ps = channels_first(z_hat, cb)
-                out_cb = work.tile([P, T], F32, name="out_cb")
+                back_ps = channels_first(z_hat[r], cb)
+                out_cb = thrice.tile([P, T], F32, name="out_cb")
                 nc.scalar.activation(
                     out_cb[:], back_ps[:], FUNC.Identity,
                     bias=column(SHIFT1, cb), scale=column(GAIN1, cb),
                 )
                 nc.sync.dma_start(out[block(cb), r * T : (r + 1) * T], out_cb[:])
 
-        embedded = embed(0)
+        embed_stages = (gather, standardise_x, make_y)
+        finish_stages = (project_out, standardise_z, write_out)
+        for stage in embed_stages:
+            stage(0)
+        gather(1)
+        project_v(0)
+        for h in range(CB):
+            project_qk(0, h)
+        standardise_x(1)
+        make_y(1)
         for r in range(SEQS):
-            y, y_bf = embedded
-            q, k, v = project(y_bf)
-            if r + 1 < SEQS:
-                embedded = embed(r + 1)
-            ctx = attend(q, k, v)
-            finish(r, y, ctx)
+            for h in range(CB):
+                probabilities(r, h)
+                if r + 1 < SEQS:
+                    if h == 0:
+                        project_v(r + 1)
+                    project_qk(r + 1, h)
+                if r + 2 < SEQS and h < len(embed_stages):
+                    embed_stages[h](r + 2)
+                if r >= 1 and h >= 1:
+                    finish_stages[h - 1](r - 1)
+                context(r, h)
+        for stage in finish_stages:
+            stage(SEQS - 1)

@@ -132,7 +132,7 @@ def tile_ternaryberttiny_b_kernel(
                     bias=column(SHIFT0, cb), scale=column(GAIN0, cb),
                 )
                 y_bf_cb = twice.tile([P, T], BF16, name=f"y_bf{cb}")
-                nc.gpsimd.tensor_copy(y_bf_cb[:], y_cb[:])
+                nc.vector.tensor_copy(y_bf_cb[:], y_cb[:])
                 y[r].append(y_cb)
                 y_bf[r].append(y_bf_cb)
 
@@ -188,7 +188,7 @@ def tile_ternaryberttiny_b_kernel(
                 one_over_sum = ring.tile([P, 1], F32, name="one_over_sum")
                 nc.vector.reciprocal(one_over_sum[:], e_sum[:])
                 p = ring.tile([P, T], BF16, name="p")
-                nc.gpsimd.tensor_scalar(p[:], e[:], one_over_sum[:], 1.0, ALU.mult, ALU.mult)
+                nc.vector.tensor_scalar_mul(p[:], e[:], one_over_sum[:])
                 p_ps = flip_p.tile([P, TB, P], BF16, name="p_ps")
                 for ub in range(TB):
                     nc.tensor.transpose(p_ps[:, ub, :], p[:, block(ub)], ident_bf16[:])

@@ -19,6 +19,14 @@ EPS = 1e-5
 SCORE_SCALE = P**-0.5
 GAIN0, SHIFT0, BQ, BO, GAIN1, SHIFT1 = 0, 1, 2, 3, 4, 5
 
+STEPS = SEQS * CB
+PROJECT_LEAD = CB
+Y_LEAD = PROJECT_LEAD + TB
+EMBED_LEAD = Y_LEAD + 1
+RESIDUAL_LAG = CB
+NORM_LAG = RESIDUAL_LAG + 1
+STORE_LAG = NORM_LAG + 1
+
 FLOPS = 4 * 2 * C * C * N + 2 * 2 * SEQS * CB * T * T * P
 
 
@@ -32,10 +40,9 @@ def tile_ternaryberttiny_b_kernel(
     nc = tc.nc
     with ExitStack() as pools:
         held = pools.enter_context(tc.tile_pool(name="held", bufs=1))
-        once = pools.enter_context(tc.tile_pool(name="once", bufs=1))
-        twice = pools.enter_context(tc.tile_pool(name="twice", bufs=2))
         thrice = pools.enter_context(tc.tile_pool(name="thrice", bufs=3))
         ring = pools.enter_context(tc.tile_pool(name="ring", bufs=4))
+        waiting = pools.enter_context(tc.tile_pool(name="waiting", bufs=2 * CB + 1))
         flip_ln = pools.enter_context(tc.psum_pool(name="flip_ln", bufs=2))
         product = pools.enter_context(tc.psum_pool(name="product", bufs=2))
         score = pools.enter_context(tc.psum_pool(name="score", bufs=2))
@@ -51,8 +58,8 @@ def tile_ternaryberttiny_b_kernel(
 
         rows = held.tile([P, C], F32, name="rows")
         nc.vector.memset(rows[:], 0.0)
-        for k, vector in enumerate((gain0, shift0, bq, bo, gain1, shift1)):
-            nc.scalar.dma_start(rows[k : k + 1, :], vector.rearrange("c one -> one c"))
+        for i, vector in enumerate((gain0, shift0, bq, bo, gain1, shift1)):
+            nc.scalar.dma_start(rows[i : i + 1, :], vector.rearrange("c one -> one c"))
         bv_rows = held.tile([P, C], F32, name="bv_rows")
         nc.scalar.dma_start(bv_rows[:], bv.rearrange("c one -> (c one)").partition_broadcast(P))
         weights = {}
@@ -73,107 +80,95 @@ def tile_ternaryberttiny_b_kernel(
         cols = held.tile([P, C], F32, name="cols")
         nc.vector.tensor_copy(cols[:], cols_ps[:])
 
-        def column(k, cb):
-            return cols[:, cb * P + k : cb * P + k + 1]
+        def column(i, cb):
+            return cols[:, cb * P + i : cb * P + i + 1]
 
-        x, x_hat, y, y_bf = {}, {}, {}, {}
-        q, k, v, p_flipped, ctx = {}, {}, {}, {}, {}
-        z, z_hat = {}, {}
+        out_blocks = out.rearrange("(cb p) j -> p cb j", p=P)
 
-        def standardise(a, name):
-            flipped = []
-            for tb in range(TB):
-                a_ps = flip_ln.tile([P, C], F32, name="a_ps")
-                for cb in range(CB):
-                    nc.tensor.transpose(a_ps[:, block(cb)], a[cb][:, block(tb)], ident_f32[:])
-                a_sb = ring.tile([P, C], F32, name="a_sb")
-                nc.scalar.copy(a_sb[:], a_ps[:])
-                stats = ring.tile([P, 6], F32, name="stats")
-                nc.vector.bn_stats(stats[:], a_sb[:])
-                mean_var = ring.tile([P, 2], F32, name="mean_var")
-                nc.vector.bn_aggr(mean_var[:], stats[:])
-                var_eps = ring.tile([P, 1], F32, name="var_eps")
-                nc.vector.tensor_scalar_add(var_eps[:], mean_var[:, 1:2], EPS)
-                rstd = ring.tile([P, 1], F32, name="rstd")
-                nc.gpsimd.tensor_tensor(rstd[:], var_eps[:], minus_half[:], ALU.pow)
-                a_hat = once.tile([P, C], F32, name=f"{name}{tb}")
-                nc.vector.tensor_scalar(
-                    a_hat[:], a_sb[:], mean_var[:, 0:1], rstd[:], ALU.subtract, ALU.mult
-                )
-                flipped.append(a_hat)
-            return flipped
+        y, y_bf = {}, {}
+        x_hat, q, k, v, p_flipped, ctx, z, z_hat = {}, {}, {}, {}, {}, {}, {}, {}
 
-        def channels_first(flipped, cb):
-            back_ps = product.tile([P, T], F32, name="back_ps", tag="product")
-            for tb in range(TB):
-                nc.tensor.transpose(back_ps[:, block(tb)], flipped[tb][:, block(cb)], ident_f32[:])
+        def standardised(a, name):
+            a_ps = flip_ln.tile([P, C], F32, name="a_ps")
+            for cb in range(CB):
+                nc.tensor.transpose(a_ps[:, block(cb)], a[:, cb, :], ident_f32[:])
+            a_sb = ring.tile([P, C], F32, name="a_sb")
+            nc.scalar.copy(a_sb[:], a_ps[:])
+            stats = ring.tile([P, 6], F32, name="stats")
+            nc.vector.bn_stats(stats[:], a_sb[:])
+            mean_var = ring.tile([P, 2], F32, name="mean_var")
+            nc.vector.bn_aggr(mean_var[:], stats[:])
+            var_eps = ring.tile([P, 1], F32, name="var_eps")
+            nc.vector.tensor_scalar_add(var_eps[:], mean_var[:, 1:2], EPS)
+            rstd = ring.tile([P, 1], F32, name="rstd")
+            nc.gpsimd.tensor_tensor(rstd[:], var_eps[:], minus_half[:], ALU.pow)
+            a_hat = thrice.tile([P, C], F32, name=name)
+            nc.vector.tensor_scalar(
+                a_hat[:], a_sb[:], mean_var[:, 0:1], rstd[:], ALU.subtract, ALU.mult
+            )
+            return a_hat
+
+        def channels_first(a_hat):
+            back_ps = product.tile([P, CB, P], F32, name="back_ps", tag="product")
+            for cb in range(CB):
+                nc.tensor.transpose(back_ps[:, cb, :], a_hat[:, block(cb)], ident_f32[:])
             return back_ps
 
-        def gather(r):
-            piece = offsets[:, r * (T // 16) : (r + 1) * (T // 16)]
-            x[r] = []
+        def embed(j):
+            tb = j % TB
+            piece = offsets[:, j * (P // 16) : (j + 1) * (P // 16)]
+            x = ring.tile([P, CB, P], F32, name="x")
             for cb in range(CB):
-                x_cb = twice.tile([P, T], F32, name=f"x{cb}")
                 nc.vector.tensor_tensor(
-                    x_cb[:], tok_sb[cb][:].indirect(piece), pos_sb[cb][:], ALU.add
+                    x[:, cb, :], tok_sb[cb][:].indirect(piece), pos_sb[cb][:, block(tb)], ALU.add
                 )
-                x[r].append(x_cb)
+            x_hat[j] = standardised(x, "x_hat")
 
-        def standardise_x(r):
-            x_hat[r] = standardise(x[r], "x_hat")
-
-        def make_y(r):
-            y[r], y_bf[r] = [], []
+        def make_y(j):
+            r, tb = divmod(j, TB)
+            if tb == 0:
+                y[r] = ring.tile([P, CB, T], F32, name="y")
+                y_bf[r] = thrice.tile([P, CB, T], BF16, name="y_bf")
+            back_ps = channels_first(x_hat[j])
             for cb in range(CB):
-                back_ps = channels_first(x_hat[r], cb)
-                y_cb = thrice.tile([P, T], F32, name=f"y{cb}")
                 nc.scalar.activation(
-                    y_cb[:], back_ps[:], FUNC.Identity,
+                    y[r][:, cb, block(tb)], back_ps[:, cb, :], FUNC.Identity,
                     bias=column(SHIFT0, cb), scale=column(GAIN0, cb),
                 )
-                y_bf_cb = twice.tile([P, T], BF16, name=f"y_bf{cb}")
-                nc.vector.tensor_copy(y_bf_cb[:], y_cb[:])
-                y[r].append(y_cb)
-                y_bf[r].append(y_bf_cb)
+            nc.vector.tensor_copy(y_bf[r][:, :, block(tb)], y[r][:, :, block(tb)])
 
-        def project_v(r):
-            v[r] = []
-            for tb in range(TB):
-                v_ps = product.tile([P, C], F32, name="v_ps", tag="product")
-                for cb in range(CB):
-                    nc.tensor.matmul(
-                        v_ps[:], y_bf[r][cb][:, block(tb)], weights["v"][:, cb, :],
-                        start=cb == 0, stop=cb == CB - 1,
-                    )
-                v_tb = twice.tile([P, C], BF16, name=f"v{tb}")
-                nc.vector.tensor_tensor(v_tb[:], v_ps[:], bv_rows[:], ALU.add)
-                v[r].append(v_tb)
-
-        def project_qk(r, h):
+        def project(j):
+            r, b = divmod(j, CB)
+            v_ps = product.tile([P, C], F32, name="v_ps", tag="product")
+            for cb in range(CB):
+                nc.tensor.matmul(
+                    v_ps[:], y_bf[r][:, cb, block(b)], weights["v"][:, cb, :],
+                    start=cb == 0, stop=cb == CB - 1,
+                )
+            v[j] = waiting.tile([P, C], BF16, name="v")
+            nc.vector.tensor_tensor(v[j][:], v_ps[:], bv_rows[:], ALU.add)
             q_ps = product.tile([P, T], F32, name="q_ps", tag="product")
             for cb in range(CB):
                 nc.tensor.matmul(
-                    q_ps[:], weights["q"][:, cb, block(h)], y_bf[r][cb][:],
+                    q_ps[:], weights["q"][:, cb, block(b)], y_bf[r][:, cb, :],
                     start=cb == 0, stop=cb == CB - 1,
                 )
-            q[r, h] = twice.tile([P, T], BF16, name=f"q{h}")
-            nc.scalar.activation(q[r, h][:], q_ps[:], FUNC.Identity, bias=column(BQ, h))
+            q[j] = waiting.tile([P, T], BF16, name="q")
+            nc.scalar.activation(q[j][:], q_ps[:], FUNC.Identity, bias=column(BQ, b))
             k_ps = product.tile([P, T], F32, name="k_ps", tag="product")
             for cb in range(CB):
                 nc.tensor.matmul(
-                    k_ps[:], weights["k"][:, cb, block(h)], y_bf[r][cb][:],
+                    k_ps[:], weights["k"][:, cb, block(b)], y_bf[r][:, cb, :],
                     start=cb == 0, stop=cb == CB - 1,
                 )
-            k[r, h] = twice.tile([P, T], BF16, name=f"k{h}")
-            nc.scalar.copy(k[r, h][:], k_ps[:])
+            k[j] = waiting.tile([P, T], BF16, name="k")
+            nc.scalar.copy(k[j][:], k_ps[:])
 
-        def probabilities(r, h):
-            p_flipped[r, h] = thrice.tile([P, TB, T], BF16, name="p_flipped")
+        def probabilities(j):
+            p_flipped[j] = thrice.tile([P, TB, T], BF16, name="p_flipped")
             for tb in range(TB):
                 s_ps = score.tile([P, T], F32, name="s_ps")
-                nc.tensor.matmul(
-                    s_ps[:], q[r, h][:, block(tb)], k[r, h][:], start=True, stop=True
-                )
+                nc.tensor.matmul(s_ps[:], q[j][:, block(tb)], k[j][:], start=True, stop=True)
                 minus_s = ring.tile([P, T], F32, name="minus_s")
                 minus_max = ring.tile([P, 1], F32, name="minus_max")
                 nc.vector.tensor_scalar(
@@ -192,67 +187,65 @@ def tile_ternaryberttiny_b_kernel(
                 p_ps = flip_p.tile([P, TB, P], BF16, name="p_ps")
                 for ub in range(TB):
                     nc.tensor.transpose(p_ps[:, ub, :], p[:, block(ub)], ident_bf16[:])
-                nc.vector.tensor_copy(p_flipped[r, h][:, :, block(tb)], p_ps[:])
+                nc.vector.tensor_copy(p_flipped[j][:, :, block(tb)], p_ps[:])
 
-        def context(r, h):
+        def context(j):
+            r, h = divmod(j, CB)
             ctx_ps = product.tile([P, T], F32, name="ctx_ps", tag="product")
             for ub in range(TB):
                 nc.tensor.matmul(
-                    ctx_ps[:], v[r][ub][:, block(h)], p_flipped[r, h][:, ub, :],
+                    ctx_ps[:], v[r * TB + ub][:, block(h)], p_flipped[j][:, ub, :],
                     start=ub == 0, stop=ub == TB - 1,
                 )
-            ctx[r, h] = twice.tile([P, T], BF16, name=f"ctx{h}")
-            nc.scalar.copy(ctx[r, h][:], ctx_ps[:])
+            ctx[j] = waiting.tile([P, T], BF16, name="ctx")
+            nc.scalar.copy(ctx[j][:], ctx_ps[:])
 
-        def project_out(r):
-            z[r] = []
+        def add_residual(j):
+            r, tb = divmod(j, TB)
+            o_ps = product.tile([P, CB, P], F32, name="o_ps", tag="product")
+            z[j] = thrice.tile([P, CB, P], F32, name="z")
             for mb in range(CB):
-                o_ps = product.tile([P, T], F32, name="o_ps", tag="product")
                 for cb in range(CB):
                     nc.tensor.matmul(
-                        o_ps[:], weights["o"][:, cb, block(mb)], ctx[r, cb][:],
+                        o_ps[:, mb, :], weights["o"][:, cb, block(mb)], ctx[r * CB + cb][:, block(tb)],
                         start=cb == 0, stop=cb == CB - 1,
                     )
-                z_mb = once.tile([P, T], F32, name=f"z{mb}")
+            for mb in range(CB):
                 nc.vector.scalar_tensor_tensor(
-                    z_mb[:], o_ps[:], column(BO, mb), y[r][mb][:], ALU.add, ALU.add
+                    z[j][:, mb, :], o_ps[:, mb, :], column(BO, mb), y[r][:, mb, block(tb)],
+                    ALU.add, ALU.add,
                 )
-                z[r].append(z_mb)
 
-        def standardise_z(r):
-            z_hat[r] = standardise(z[r], "z_hat")
+        def standardise_z(j):
+            z_hat[j] = standardised(z[j], "z_hat")
 
-        def write_out(r):
+        def write_out(j):
+            back_ps = channels_first(z_hat[j])
+            out_sb = thrice.tile([P, CB, P], F32, name="out_sb")
             for cb in range(CB):
-                back_ps = channels_first(z_hat[r], cb)
-                out_cb = thrice.tile([P, T], F32, name="out_cb")
                 nc.scalar.activation(
-                    out_cb[:], back_ps[:], FUNC.Identity,
+                    out_sb[:, cb, :], back_ps[:, cb, :], FUNC.Identity,
                     bias=column(SHIFT1, cb), scale=column(GAIN1, cb),
                 )
-                nc.sync.dma_start(out[block(cb), r * T : (r + 1) * T], out_cb[:])
+            nc.sync.dma_start(out_blocks[:, :, block(j)], out_sb[:])
 
-        embed_stages = (gather, standardise_x, make_y)
-        finish_stages = (project_out, standardise_z, write_out)
-        for stage in embed_stages:
-            stage(0)
-        gather(1)
-        project_v(0)
-        for h in range(CB):
-            project_qk(0, h)
-        standardise_x(1)
-        make_y(1)
-        for r in range(SEQS):
-            for h in range(CB):
-                probabilities(r, h)
-                if r + 1 < SEQS:
-                    if h == 0:
-                        project_v(r + 1)
-                    project_qk(r + 1, h)
-                if r + 2 < SEQS and h < len(embed_stages):
-                    embed_stages[h](r + 2)
-                if r >= 1 and h >= 1:
-                    finish_stages[h - 1](r - 1)
-                context(r, h)
-        for stage in finish_stages:
-            stage(SEQS - 1)
+        def valid(j):
+            return 0 <= j < STEPS
+
+        for step in range(-EMBED_LEAD, STEPS + STORE_LAG):
+            if valid(step):
+                probabilities(step)
+            if valid(step - RESIDUAL_LAG):
+                add_residual(step - RESIDUAL_LAG)
+            if valid(step + EMBED_LEAD):
+                embed(step + EMBED_LEAD)
+            if valid(step - NORM_LAG):
+                standardise_z(step - NORM_LAG)
+            if valid(step + PROJECT_LEAD):
+                project(step + PROJECT_LEAD)
+            if valid(step + Y_LEAD):
+                make_y(step + Y_LEAD)
+            if valid(step - STORE_LAG):
+                write_out(step - STORE_LAG)
+            if valid(step):
+                context(step)

@@ -187,7 +187,7 @@ def tile_ternaryberttiny_b_kernel(
                 p_ps = flip_p.tile([P, TB, P], BF16, name="p_ps")
                 for ub in range(TB):
                     nc.tensor.transpose(p_ps[:, ub, :], p[:, block(ub)], ident_bf16[:])
-                nc.vector.tensor_copy(p_flipped[j][:, :, block(tb)], p_ps[:])
+                nc.scalar.copy(p_flipped[j][:, :, block(tb)], p_ps[:])
 
         def context(j):
             r, h = divmod(j, CB)

@@ -43,8 +43,8 @@ def tile_ternaryberttiny_b_kernel(
         thrice = pools.enter_context(tc.tile_pool(name="thrice", bufs=3))
         ring = pools.enter_context(tc.tile_pool(name="ring", bufs=4))
         waiting = pools.enter_context(tc.tile_pool(name="waiting", bufs=2 * CB + 1))
-        flip_ln = pools.enter_context(tc.psum_pool(name="flip_ln", bufs=2))
-        product = pools.enter_context(tc.psum_pool(name="product", bufs=2))
+        flip_ln = pools.enter_context(tc.psum_pool(name="flip_ln", bufs=1))
+        product = pools.enter_context(tc.psum_pool(name="product", bufs=3))
         score = pools.enter_context(tc.psum_pool(name="score", bufs=2))
         flip_p = pools.enter_context(tc.psum_pool(name="flip_p", bufs=2))
 

@@ -17,7 +17,6 @@ CB = C // P
 TB = T // P
 EPS = 1e-5
 SCORE_SCALE = P**-0.5
-GAIN0, SHIFT0, BQ, BO, GAIN1, SHIFT1 = 0, 1, 2, 3, 4, 5
 
 STEPS = SEQS * CB
 PROJECT_LEAD = CB
@@ -43,7 +42,7 @@ def tile_ternaryberttiny_b_kernel(
         thrice = pools.enter_context(tc.tile_pool(name="thrice", bufs=3))
         ring = pools.enter_context(tc.tile_pool(name="ring", bufs=4))
         waiting = pools.enter_context(tc.tile_pool(name="waiting", bufs=2 * CB + 1))
-        flip_ln = pools.enter_context(tc.psum_pool(name="flip_ln", bufs=1))
+        flip_x = pools.enter_context(tc.psum_pool(name="flip_x", bufs=1))
         product = pools.enter_context(tc.psum_pool(name="product", bufs=3))
         score = pools.enter_context(tc.psum_pool(name="score", bufs=2))
         flip_p = pools.enter_context(tc.psum_pool(name="flip_p", bufs=2))
@@ -56,16 +55,33 @@ def tile_ternaryberttiny_b_kernel(
             nc.sync.dma_start(tok_sb[cb][:], tok[block(cb), :])
             nc.scalar.dma_start(pos_sb[cb][:], pos[block(cb), :])
 
-        rows = held.tile([P, C], F32, name="rows")
-        nc.vector.memset(rows[:], 0.0)
-        for i, vector in enumerate((gain0, shift0, bq, bo, gain1, shift1)):
-            nc.scalar.dma_start(rows[i : i + 1, :], vector.rearrange("c one -> one c"))
-        bv_rows = held.tile([P, C], F32, name="bv_rows")
-        nc.scalar.dma_start(bv_rows[:], bv.rearrange("c one -> (c one)").partition_broadcast(P))
+        def in_every_partition(vector, name):
+            row = held.tile([P, C], F32, name=name)
+            nc.sync.dma_start(row[:], vector.rearrange("c one -> (c one)").partition_broadcast(P))
+            return row
+
+        def one_to_a_partition(vector, name):
+            column = held.tile([P, CB], F32, name=name)
+            nc.scalar.dma_start(column[:], vector.rearrange("(cb p) one -> p (cb one)", p=P))
+            return column
+
+        gain0_row = in_every_partition(gain0, "gain0_row")
+        shift0_row = in_every_partition(shift0, "shift0_row")
+        bo_row = in_every_partition(bo, "bo_row")
+        bo_col = one_to_a_partition(bo, "bo_col")
+        bv_row = in_every_partition(bv, "bv_row")
+        bq_col = one_to_a_partition(bq, "bq_col")
         weights = {}
         for name, w in (("v", wv), ("q", wq), ("k", wk), ("o", wo)):
             weights[name] = held.tile([P, CB, C], BF16, name=f"w{name}")
             nc.sync.dma_start(weights[name][:], w.rearrange("(cb p) m -> p cb m", p=P))
+        gain1_col = one_to_a_partition(gain1, "gain1_col")
+        shift1_col = one_to_a_partition(shift1, "shift1_col")
+
+        shift0_bo_row = held.tile([P, C], F32, name="shift0_bo_row")
+        nc.gpsimd.tensor_tensor(shift0_bo_row[:], shift0_row[:], bo_row[:], ALU.add)
+        minus_bo_col = held.tile([P, CB], F32, name="minus_bo_col")
+        nc.gpsimd.tensor_scalar_mul(minus_bo_col[:], bo_col[:], -1.0)
 
         ident_f32 = held.tile([P, P], F32, name="ident_f32")
         make_identity(nc, ident_f32[:])
@@ -74,44 +90,26 @@ def tile_ternaryberttiny_b_kernel(
         minus_half = held.tile([P, 1], F32, name="minus_half")
         nc.vector.memset(minus_half[:], -0.5)
 
-        cols_ps = product.tile([P, C], F32, name="cols_ps", tag="product")
-        for cb in range(CB):
-            nc.tensor.transpose(cols_ps[:, block(cb)], rows[:, block(cb)], ident_f32[:])
-        cols = held.tile([P, C], F32, name="cols")
-        nc.vector.tensor_copy(cols[:], cols_ps[:])
-
-        def column(i, cb):
-            return cols[:, cb * P + i : cb * P + i + 1]
-
         out_blocks = out.rearrange("(cb p) j -> p cb j", p=P)
 
-        y, y_bf = {}, {}
-        x_hat, q, k, v, p_flipped, ctx, z, z_hat = {}, {}, {}, {}, {}, {}, {}, {}
+        y_bf = {}
+        y_bo, q, k, v, p_flipped, ctx, z, z_hat = {}, {}, {}, {}, {}, {}, {}, {}
 
-        def standardised(a, name):
-            a_ps = flip_ln.tile([P, C], F32, name="a_ps")
-            for cb in range(CB):
-                nc.tensor.transpose(a_ps[:, block(cb)], a[:, cb, :], ident_f32[:])
-            a_sb = ring.tile([P, C], F32, name="a_sb")
-            nc.scalar.copy(a_sb[:], a_ps[:])
+        def moments(a):
             stats = ring.tile([P, 6], F32, name="stats")
-            nc.vector.bn_stats(stats[:], a_sb[:])
+            nc.vector.bn_stats(stats[:], a[:])
             mean_var = ring.tile([P, 2], F32, name="mean_var")
             nc.vector.bn_aggr(mean_var[:], stats[:])
             var_eps = ring.tile([P, 1], F32, name="var_eps")
             nc.vector.tensor_scalar_add(var_eps[:], mean_var[:, 1:2], EPS)
             rstd = ring.tile([P, 1], F32, name="rstd")
             nc.gpsimd.tensor_tensor(rstd[:], var_eps[:], minus_half[:], ALU.pow)
-            a_hat = thrice.tile([P, C], F32, name=name)
-            nc.vector.tensor_scalar(
-                a_hat[:], a_sb[:], mean_var[:, 0:1], rstd[:], ALU.subtract, ALU.mult
-            )
-            return a_hat
+            return mean_var[:, 0:1], rstd[:]
 
-        def channels_first(a_hat):
+        def channels_first(a):
             back_ps = product.tile([P, CB, P], F32, name="back_ps", tag="product")
             for cb in range(CB):
-                nc.tensor.transpose(back_ps[:, cb, :], a_hat[:, block(cb)], ident_f32[:])
+                nc.tensor.transpose(back_ps[:, cb, :], a[:, block(cb)], ident_f32[:])
             return back_ps
 
         def embed(j):
@@ -122,20 +120,31 @@ def tile_ternaryberttiny_b_kernel(
                 nc.vector.tensor_tensor(
                     x[:, cb, :], tok_sb[cb][:].indirect(piece), pos_sb[cb][:, block(tb)], ALU.add
                 )
-            x_hat[j] = standardised(x, "x_hat")
+            x_ps = flip_x.tile([P, C], F32, name="x_ps")
+            for cb in range(CB):
+                nc.tensor.transpose(x_ps[:, block(cb)], x[:, cb, :], ident_f32[:])
+            x_rows = ring.tile([P, C], F32, name="x_rows")
+            nc.scalar.copy(x_rows[:], x_ps[:])
+            mean, rstd = moments(x_rows)
+            centred = ring.tile([P, C], F32, name="centred")
+            nc.vector.scalar_tensor_tensor(
+                centred[:], x_rows[:], mean, gain0_row[:], ALU.subtract, ALU.mult
+            )
+            y_bo[j] = held.tile([P, C], F32, name=f"y_bo{j}")
+            nc.vector.scalar_tensor_tensor(
+                y_bo[j][:], centred[:], rstd, shift0_bo_row[:], ALU.mult, ALU.add
+            )
 
         def make_y(j):
             r, tb = divmod(j, TB)
             if tb == 0:
-                y[r] = ring.tile([P, CB, T], F32, name="y")
                 y_bf[r] = thrice.tile([P, CB, T], BF16, name="y_bf")
-            back_ps = channels_first(x_hat[j])
+            back_ps = channels_first(y_bo[j])
             for cb in range(CB):
                 nc.scalar.activation(
-                    y[r][:, cb, block(tb)], back_ps[:, cb, :], FUNC.Identity,
-                    bias=column(SHIFT0, cb), scale=column(GAIN0, cb),
+                    y_bf[r][:, cb, block(tb)], back_ps[:, cb, :], FUNC.Identity,
+                    bias=minus_bo_col[:, cb : cb + 1],
                 )
-            nc.vector.tensor_copy(y_bf[r][:, :, block(tb)], y[r][:, :, block(tb)])
 
         def project(j):
             r, b = divmod(j, CB)
@@ -146,7 +155,7 @@ def tile_ternaryberttiny_b_kernel(
                     start=cb == 0, stop=cb == CB - 1,
                 )
             v[j] = waiting.tile([P, C], BF16, name="v")
-            nc.vector.tensor_tensor(v[j][:], v_ps[:], bv_rows[:], ALU.add)
+            nc.vector.tensor_tensor(v[j][:], v_ps[:], bv_row[:], ALU.add)
             q_ps = product.tile([P, T], F32, name="q_ps", tag="product")
             for cb in range(CB):
                 nc.tensor.matmul(
@@ -154,7 +163,7 @@ def tile_ternaryberttiny_b_kernel(
                     start=cb == 0, stop=cb == CB - 1,
                 )
             q[j] = waiting.tile([P, T], BF16, name="q")
-            nc.scalar.activation(q[j][:], q_ps[:], FUNC.Identity, bias=column(BQ, b))
+            nc.scalar.activation(q[j][:], q_ps[:], FUNC.Identity, bias=bq_col[:, b : b + 1])
             k_ps = product.tile([P, T], F32, name="k_ps", tag="product")
             for cb in range(CB):
                 nc.tensor.matmul(
@@ -202,22 +211,19 @@ def tile_ternaryberttiny_b_kernel(
 
         def add_residual(j):
             r, tb = divmod(j, TB)
-            o_ps = product.tile([P, CB, P], F32, name="o_ps", tag="product")
-            z[j] = thrice.tile([P, CB, P], F32, name="z")
-            for mb in range(CB):
-                for cb in range(CB):
-                    nc.tensor.matmul(
-                        o_ps[:, mb, :], weights["o"][:, cb, block(mb)], ctx[r * CB + cb][:, block(tb)],
-                        start=cb == 0, stop=cb == CB - 1,
-                    )
-            for mb in range(CB):
-                nc.vector.scalar_tensor_tensor(
-                    z[j][:, mb, :], o_ps[:, mb, :], column(BO, mb), y[r][:, mb, block(tb)],
-                    ALU.add, ALU.add,
+            o_ps = product.tile([P, C], F32, name="o_ps", tag="product")
+            for cb in range(CB):
+                nc.tensor.matmul(
+                    o_ps[:], ctx[r * CB + cb][:, block(tb)], weights["o"][:, cb, :],
+                    start=cb == 0, stop=cb == CB - 1,
                 )
+            z[j] = thrice.tile([P, C], F32, name="z")
+            nc.vector.tensor_tensor(z[j][:], o_ps[:], y_bo[j][:], ALU.add)
 
         def standardise_z(j):
-            z_hat[j] = standardised(z[j], "z_hat")
+            mean, rstd = moments(z[j])
+            z_hat[j] = thrice.tile([P, C], F32, name="z_hat")
+            nc.vector.tensor_scalar(z_hat[j][:], z[j][:], mean, rstd, ALU.subtract, ALU.mult)
 
         def write_out(j):
             back_ps = channels_first(z_hat[j])
@@ -225,7 +231,7 @@ def tile_ternaryberttiny_b_kernel(
             for cb in range(CB):
                 nc.scalar.activation(
                     out_sb[:, cb, :], back_ps[:, cb, :], FUNC.Identity,
-                    bias=column(SHIFT1, cb), scale=column(GAIN1, cb),
+                    bias=shift1_col[:, cb : cb + 1], scale=gain1_col[:, cb : cb + 1],
                 )
             nc.sync.dma_start(out_blocks[:, :, block(j)], out_sb[:])
 

@@ -19,8 +19,9 @@ EPS = 1e-5
 SCORE_SCALE = P**-0.5
 
 STEPS = SEQS * CB
-PROJECT_LEAD = CB
-Y_LEAD = PROJECT_LEAD + TB
+QK_LEAD = 1
+Y_LEAD = QK_LEAD + TB
+V_LEAD = Y_LEAD - 1
 EMBED_LEAD = Y_LEAD + 1
 RESIDUAL_LAG = CB
 NORM_LAG = RESIDUAL_LAG + 1
@@ -42,6 +43,7 @@ def tile_ternaryberttiny_b_kernel(
         thrice = pools.enter_context(tc.tile_pool(name="thrice", bufs=3))
         ring = pools.enter_context(tc.tile_pool(name="ring", bufs=4))
         waiting = pools.enter_context(tc.tile_pool(name="waiting", bufs=2 * CB + 1))
+        long_waiting = pools.enter_context(tc.tile_pool(name="long_waiting", bufs=3 * TB + 1))
         flip_x = pools.enter_context(tc.psum_pool(name="flip_x", bufs=1))
         product = pools.enter_context(tc.psum_pool(name="product", bufs=3))
         score = pools.enter_context(tc.psum_pool(name="score", bufs=2))
@@ -106,8 +108,8 @@ def tile_ternaryberttiny_b_kernel(
             nc.gpsimd.tensor_tensor(rstd[:], var_eps[:], minus_half[:], ALU.pow)
             return mean_var[:, 0:1], rstd[:]
 
-        def channels_first(a):
-            back_ps = product.tile([P, CB, P], F32, name="back_ps", tag="product")
+        def channels_first(a, pool, tag):
+            back_ps = pool.tile([P, CB, P], F32, name="back_ps", tag=tag)
             for cb in range(CB):
                 nc.tensor.transpose(back_ps[:, cb, :], a[:, block(cb)], ident_f32[:])
             return back_ps
@@ -139,23 +141,26 @@ def tile_ternaryberttiny_b_kernel(
             r, tb = divmod(j, TB)
             if tb == 0:
                 y_bf[r] = thrice.tile([P, CB, T], BF16, name="y_bf")
-            back_ps = channels_first(y_bo[j])
+            back_ps = channels_first(y_bo[j], product, "product")
             for cb in range(CB):
                 nc.scalar.activation(
                     y_bf[r][:, cb, block(tb)], back_ps[:, cb, :], FUNC.Identity,
                     bias=minus_bo_col[:, cb : cb + 1],
                 )
 
-        def project(j):
-            r, b = divmod(j, CB)
+        def project_v(j):
+            r, b = divmod(j, TB)
             v_ps = product.tile([P, C], F32, name="v_ps", tag="product")
             for cb in range(CB):
                 nc.tensor.matmul(
                     v_ps[:], y_bf[r][:, cb, block(b)], weights["v"][:, cb, :],
                     start=cb == 0, stop=cb == CB - 1,
                 )
-            v[j] = waiting.tile([P, C], BF16, name="v")
+            v[j] = long_waiting.tile([P, C], BF16, name="v")
             nc.vector.tensor_tensor(v[j][:], v_ps[:], bv_row[:], ALU.add)
+
+        def project_qk(j):
+            r, b = divmod(j, CB)
             q_ps = product.tile([P, T], F32, name="q_ps", tag="product")
             for cb in range(CB):
                 nc.tensor.matmul(
@@ -226,7 +231,7 @@ def tile_ternaryberttiny_b_kernel(
             nc.vector.tensor_scalar(z_hat[j][:], z[j][:], mean, rstd, ALU.subtract, ALU.mult)
 
         def write_out(j):
-            back_ps = channels_first(z_hat[j])
+            back_ps = channels_first(z_hat[j], flip_x, "x_ps")
             out_sb = thrice.tile([P, CB, P], F32, name="out_sb")
             for cb in range(CB):
                 nc.scalar.activation(
@@ -247,10 +252,12 @@ def tile_ternaryberttiny_b_kernel(
                 embed(step + EMBED_LEAD)
             if valid(step - NORM_LAG):
                 standardise_z(step - NORM_LAG)
-            if valid(step + PROJECT_LEAD):
-                project(step + PROJECT_LEAD)
+            if valid(step + QK_LEAD):
+                project_qk(step + QK_LEAD)
             if valid(step + Y_LEAD):
                 make_y(step + Y_LEAD)
+            if valid(step + V_LEAD):
+                project_v(step + V_LEAD)
             if valid(step - STORE_LAG):
                 write_out(step - STORE_LAG)
             if valid(step):

@@ -71,7 +71,7 @@ def tile_ternaryberttiny_b_kernel(
         shift0_row = in_every_partition(shift0, "shift0_row")
         bo_row = in_every_partition(bo, "bo_row")
         bo_col = one_to_a_partition(bo, "bo_col")
-        bv_row = in_every_partition(bv, "bv_row")
+        bv_col = one_to_a_partition(bv, "bv_col")
         bq_col = one_to_a_partition(bq, "bq_col")
         weights = {}
         for name, w in (("v", wv), ("q", wq), ("k", wk), ("o", wo)):
@@ -157,7 +157,7 @@ def tile_ternaryberttiny_b_kernel(
                     start=cb == 0, stop=cb == CB - 1,
                 )
             v[j] = long_waiting.tile([P, C], BF16, name="v")
-            nc.vector.tensor_tensor(v[j][:], v_ps[:], bv_row[:], ALU.add)
+            nc.scalar.copy(v[j][:], v_ps[:])
 
         def project_qk(j):
             r, b = divmod(j, CB)
@@ -212,7 +212,7 @@ def tile_ternaryberttiny_b_kernel(
                     start=ub == 0, stop=ub == TB - 1,
                 )
             ctx[j] = waiting.tile([P, T], BF16, name="ctx")
-            nc.scalar.copy(ctx[j][:], ctx_ps[:])
+            nc.scalar.activation(ctx[j][:], ctx_ps[:], FUNC.Identity, bias=bv_col[:, h : h + 1])
 
         def add_residual(j):
             r, tb = divmod(j, TB)

@@ -40,6 +40,7 @@ def tile_ternaryberttiny_b_kernel(
     nc = tc.nc
     with ExitStack() as pools:
         held = pools.enter_context(tc.tile_pool(name="held", bufs=1))
+        twice = pools.enter_context(tc.tile_pool(name="twice", bufs=2))
         thrice = pools.enter_context(tc.tile_pool(name="thrice", bufs=3))
         ring = pools.enter_context(tc.tile_pool(name="ring", bufs=4))
         waiting = pools.enter_context(tc.tile_pool(name="waiting", bufs=2 * CB + 1))
@@ -94,7 +95,7 @@ def tile_ternaryberttiny_b_kernel(
 
         out_blocks = out.rearrange("(cb p) j -> p cb j", p=P)
 
-        y_bf = {}
+        x, y_bf = {}, {}
         y_bo, q, k, v, p_flipped, ctx, z, z_hat = {}, {}, {}, {}, {}, {}, {}, {}
 
         def moments(a):
@@ -115,16 +116,17 @@ def tile_ternaryberttiny_b_kernel(
             return back_ps
 
         def embed(j):
-            tb = j % TB
-            piece = offsets[:, j * (P // 16) : (j + 1) * (P // 16)]
-            x = ring.tile([P, CB, P], F32, name="x")
-            for cb in range(CB):
-                nc.vector.tensor_tensor(
-                    x[:, cb, :], tok_sb[cb][:].indirect(piece), pos_sb[cb][:, block(tb)], ALU.add
-                )
+            r, tb = divmod(j, TB)
+            if tb == 0:
+                piece = offsets[:, r * (T // 16) : (r + 1) * (T // 16)]
+                x[r] = twice.tile([P, CB, T], F32, name="x")
+                for cb in range(CB):
+                    nc.vector.tensor_tensor(
+                        x[r][:, cb, :], tok_sb[cb][:].indirect(piece), pos_sb[cb][:], ALU.add
+                    )
             x_ps = flip_x.tile([P, C], F32, name="x_ps")
             for cb in range(CB):
-                nc.tensor.transpose(x_ps[:, block(cb)], x[:, cb, :], ident_f32[:])
+                nc.tensor.transpose(x_ps[:, block(cb)], x[r][:, cb, block(tb)], ident_f32[:])
             x_rows = ring.tile([P, C], F32, name="x_rows")
             nc.scalar.copy(x_rows[:], x_ps[:])
             mean, rstd = moments(x_rows)

@@ -19,13 +19,16 @@ EPS = 1e-5
 SCORE_SCALE = P**-0.5
 
 STEPS = SEQS * CB
+LAST = SEQS - 1
 QK_LEAD = 1
+LAST_QK_LEAD = 2
 Y_LEAD = QK_LEAD + TB
 V_LEAD = Y_LEAD - 1
 EMBED_LEAD = Y_LEAD + 1
 RESIDUAL_LAG = CB
-NORM_LAG = RESIDUAL_LAG + 1
-STORE_LAG = NORM_LAG + 1
+LAST_RESIDUAL_LAG = 1
+NORM_LAG = 1
+STORE_LAG = 2
 
 FLOPS = 4 * 2 * C * C * N + 2 * 2 * SEQS * CB * T * T * P
 
@@ -180,11 +183,18 @@ def tile_ternaryberttiny_b_kernel(
             k[j] = waiting.tile([P, T], BF16, name="k")
             nc.scalar.copy(k[j][:], k_ps[:])
 
+        def attended(j):
+            r, b = divmod(j, CB)
+            return [(h, b) for h in range(CB)] if r == LAST else [(b, tb) for tb in range(TB)]
+
         def probabilities(j):
             p_flipped[j] = thrice.tile([P, TB, T], BF16, name="p_flipped")
-            for tb in range(TB):
+            for i, (h, tb) in enumerate(attended(j)):
+                head = j // CB * CB + h
                 s_ps = score.tile([P, T], F32, name="s_ps")
-                nc.tensor.matmul(s_ps[:], q[j][:, block(tb)], k[j][:], start=True, stop=True)
+                nc.tensor.matmul(
+                    s_ps[:], q[head][:, block(tb)], k[head][:], start=True, stop=True
+                )
                 minus_s = ring.tile([P, T], F32, name="minus_s")
                 minus_max = ring.tile([P, 1], F32, name="minus_max")
                 nc.vector.tensor_scalar(
@@ -203,25 +213,32 @@ def tile_ternaryberttiny_b_kernel(
                 p_ps = flip_p.tile([P, TB, P], BF16, name="p_ps")
                 for ub in range(TB):
                     nc.tensor.transpose(p_ps[:, ub, :], p[:, block(ub)], ident_bf16[:])
-                nc.scalar.copy(p_flipped[j][:, :, block(tb)], p_ps[:])
+                nc.scalar.copy(p_flipped[j][:, :, block(i)], p_ps[:])
 
         def context(j):
-            r, h = divmod(j, CB)
+            r, b = divmod(j, CB)
+            runs = [(h, block(h)) for h in range(CB)] if r == LAST else [(b, slice(0, T))]
             ctx_ps = product.tile([P, T], F32, name="ctx_ps", tag="product")
-            for ub in range(TB):
-                nc.tensor.matmul(
-                    ctx_ps[:], v[r * TB + ub][:, block(h)], p_flipped[j][:, ub, :],
-                    start=ub == 0, stop=ub == TB - 1,
-                )
             ctx[j] = waiting.tile([P, T], BF16, name="ctx")
-            nc.scalar.activation(ctx[j][:], ctx_ps[:], FUNC.Identity, bias=bv_col[:, h : h + 1])
+            for h, columns in runs:
+                for ub in range(TB):
+                    nc.tensor.matmul(
+                        ctx_ps[:, columns], v[r * TB + ub][:, block(h)], p_flipped[j][:, ub, columns],
+                        start=ub == 0, stop=ub == TB - 1,
+                    )
+            for h, columns in runs:
+                nc.scalar.activation(
+                    ctx[j][:, columns], ctx_ps[:, columns], FUNC.Identity, bias=bv_col[:, h : h + 1]
+                )
 
         def add_residual(j):
             r, tb = divmod(j, TB)
             o_ps = product.tile([P, C], F32, name="o_ps", tag="product")
             for cb in range(CB):
                 nc.tensor.matmul(
-                    o_ps[:], ctx[r * CB + cb][:, block(tb)], weights["o"][:, cb, :],
+                    o_ps[:],
+                    ctx[j][:, block(cb)] if r == LAST else ctx[r * CB + cb][:, block(tb)],
+                    weights["o"][:, cb, :],
                     start=cb == 0, stop=cb == CB - 1,
                 )
             z[j] = thrice.tile([P, C], F32, name="z")
@@ -242,25 +259,31 @@ def tile_ternaryberttiny_b_kernel(
                 )
             nc.sync.dma_start(out_blocks[:, :, block(j)], out_sb[:])
 
-        def valid(j):
-            return 0 <= j < STEPS
+        NEVER = STEPS * STEPS
 
-        for step in range(-EMBED_LEAD, STEPS + STORE_LAG):
-            if valid(step):
-                probabilities(step)
-            if valid(step - RESIDUAL_LAG):
-                add_residual(step - RESIDUAL_LAG)
-            if valid(step + EMBED_LEAD):
-                embed(step + EMBED_LEAD)
-            if valid(step - NORM_LAG):
-                standardise_z(step - NORM_LAG)
-            if valid(step + QK_LEAD):
-                project_qk(step + QK_LEAD)
-            if valid(step + Y_LEAD):
-                make_y(step + Y_LEAD)
-            if valid(step + V_LEAD):
-                project_v(step + V_LEAD)
-            if valid(step - STORE_LAG):
-                write_out(step - STORE_LAG)
-            if valid(step):
-                context(step)
+        def qk_step(j):
+            return j - QK_LEAD if j < LAST * CB else NEVER
+
+        def last_qk_step(j):
+            return NEVER if j < LAST * CB else LAST * CB - LAST_QK_LEAD + j % CB // 2
+
+        def residual_step(j):
+            return j + (LAST_RESIDUAL_LAG if j // CB == LAST else RESIDUAL_LAG)
+
+        for step in range(-EMBED_LEAD, STEPS + LAST_RESIDUAL_LAG + STORE_LAG):
+            stages = (
+                (probabilities, lambda j: j),
+                (add_residual, residual_step),
+                (embed, lambda j: j - EMBED_LEAD),
+                (standardise_z, lambda j: residual_step(j) + NORM_LAG),
+                (project_qk, qk_step),
+                (make_y, lambda j: j - Y_LEAD),
+                (project_v, lambda j: j - V_LEAD),
+                (write_out, lambda j: residual_step(j) + STORE_LAG),
+                (project_qk, last_qk_step),
+                (context, lambda j: j),
+            )
+            for stage, step_of in stages:
+                for j in range(STEPS):
+                    if step_of(j) == step:
+                        stage(j)

@@ -19,16 +19,13 @@ EPS = 1e-5
 SCORE_SCALE = P**-0.5
 
 STEPS = SEQS * CB
+PARTS = CB
 LAST = SEQS - 1
 QK_LEAD = 1
-LAST_QK_LEAD = 2
-Y_LEAD = QK_LEAD + TB
-V_LEAD = Y_LEAD - 1
-EMBED_LEAD = Y_LEAD + 1
-RESIDUAL_LAG = CB
-LAST_RESIDUAL_LAG = 1
-NORM_LAG = 1
-STORE_LAG = 2
+CTX_LAG = 2
+RESIDUAL_LAG = CTX_LAG + TB - 1
+LAST_RESIDUAL_LAG = CTX_LAG
+OUT_LAG = 2
 
 FLOPS = 4 * 2 * C * C * N + 2 * 2 * SEQS * CB * T * T * P
 
@@ -43,15 +40,13 @@ def tile_ternaryberttiny_b_kernel(
     nc = tc.nc
     with ExitStack() as pools:
         held = pools.enter_context(tc.tile_pool(name="held", bufs=1))
-        twice = pools.enter_context(tc.tile_pool(name="twice", bufs=2))
         thrice = pools.enter_context(tc.tile_pool(name="thrice", bufs=3))
         ring = pools.enter_context(tc.tile_pool(name="ring", bufs=4))
         waiting = pools.enter_context(tc.tile_pool(name="waiting", bufs=2 * CB + 1))
         long_waiting = pools.enter_context(tc.tile_pool(name="long_waiting", bufs=3 * TB + 1))
-        flip_x = pools.enter_context(tc.psum_pool(name="flip_x", bufs=1))
-        product = pools.enter_context(tc.psum_pool(name="product", bufs=3))
         score = pools.enter_context(tc.psum_pool(name="score", bufs=2))
         flip_p = pools.enter_context(tc.psum_pool(name="flip_p", bufs=2))
+        product = pools.enter_context(tc.psum_pool(name="product", bufs=4))
 
         offsets = held.tile([P, N // 16], U16, name="offsets")
         nc.sync.dma_start(offsets[:], offs)
@@ -99,7 +94,13 @@ def tile_ternaryberttiny_b_kernel(
         out_blocks = out.rearrange("(cb p) j -> p cb j", p=P)
 
         x, y_bf = {}, {}
-        y_bo, q, k, v, p_flipped, ctx, z, z_hat = {}, {}, {}, {}, {}, {}, {}, {}
+        s_ps, e, e_sum, p, p_ps = {}, {}, {}, {}, {}
+        x_ps, y_ps, q_ps, k_ps, v_ps, ctx_ps, o_ps, out_ps = {}, {}, {}, {}, {}, {}, {}, {}
+        x_rows, moments_x, y_bo, q, k, v, p_flipped, ctx = {}, {}, {}, {}, {}, {}, {}, {}
+        z, moments_z, z_hat = {}, {}, {}
+
+        def bank(name):
+            return product.tile([P, T], F32, name=name, tag="product")
 
         def moments(a):
             stats = ring.tile([P, 6], F32, name="stats")
@@ -112,178 +113,262 @@ def tile_ternaryberttiny_b_kernel(
             nc.gpsimd.tensor_tensor(rstd[:], var_eps[:], minus_half[:], ALU.pow)
             return mean_var[:, 0:1], rstd[:]
 
-        def channels_first(a, pool, tag):
-            back_ps = pool.tile([P, CB, P], F32, name="back_ps", tag=tag)
-            for cb in range(CB):
-                nc.tensor.transpose(back_ps[:, cb, :], a[:, block(cb)], ident_f32[:])
-            return back_ps
+        def look_up(j):
+            r, cb = divmod(j, CB)
+            if cb == 0:
+                x[r] = held.tile([P, CB, T], F32, name="x")
+            piece = offsets[:, r * (T // 16) : (r + 1) * (T // 16)]
+            nc.vector.tensor_tensor(
+                x[r][:, cb, :], tok_sb[cb][:].indirect(piece), pos_sb[cb][:], ALU.add
+            )
 
-        def embed(j):
+        def flip_x(j):
             r, tb = divmod(j, TB)
-            if tb == 0:
-                piece = offsets[:, r * (T // 16) : (r + 1) * (T // 16)]
-                x[r] = twice.tile([P, CB, T], F32, name="x")
-                for cb in range(CB):
-                    nc.vector.tensor_tensor(
-                        x[r][:, cb, :], tok_sb[cb][:].indirect(piece), pos_sb[cb][:], ALU.add
-                    )
-            x_ps = flip_x.tile([P, C], F32, name="x_ps")
+            x_ps[j] = bank("x_ps")
             for cb in range(CB):
-                nc.tensor.transpose(x_ps[:, block(cb)], x[r][:, cb, block(tb)], ident_f32[:])
-            x_rows = ring.tile([P, C], F32, name="x_rows")
-            nc.scalar.copy(x_rows[:], x_ps[:])
-            mean, rstd = moments(x_rows)
+                nc.tensor.transpose(x_ps[j][:, block(cb)], x[r][:, cb, block(tb)], ident_f32[:])
+
+        def keep_x(j):
+            x_rows[j] = ring.tile([P, C], F32, name="x_rows")
+            nc.scalar.copy(x_rows[j][:], x_ps[j][:])
+
+        def measure_x(j):
+            moments_x[j] = moments(x_rows[j])
+
+        def normalise_x(j):
+            mean, rstd = moments_x[j]
             centred = ring.tile([P, C], F32, name="centred")
             nc.vector.scalar_tensor_tensor(
-                centred[:], x_rows[:], mean, gain0_row[:], ALU.subtract, ALU.mult
+                centred[:], x_rows[j][:], mean, gain0_row[:], ALU.subtract, ALU.mult
             )
             y_bo[j] = held.tile([P, C], F32, name=f"y_bo{j}")
             nc.vector.scalar_tensor_tensor(
                 y_bo[j][:], centred[:], rstd, shift0_bo_row[:], ALU.mult, ALU.add
             )
 
-        def make_y(j):
+        def flip_y(j):
+            y_ps[j] = bank("y_ps")
+            for cb in range(CB):
+                nc.tensor.transpose(y_ps[j][:, block(cb)], y_bo[j][:, block(cb)], ident_f32[:])
+
+        def keep_y(j):
             r, tb = divmod(j, TB)
             if tb == 0:
                 y_bf[r] = thrice.tile([P, CB, T], BF16, name="y_bf")
-            back_ps = channels_first(y_bo[j], product, "product")
             for cb in range(CB):
                 nc.scalar.activation(
-                    y_bf[r][:, cb, block(tb)], back_ps[:, cb, :], FUNC.Identity,
+                    y_bf[r][:, cb, block(tb)], y_ps[j][:, block(cb)], FUNC.Identity,
                     bias=minus_bo_col[:, cb : cb + 1],
                 )
 
+        def project(name, ps, j):
+            r, h = divmod(j, CB)
+            ps[j] = bank(f"{name}_ps")
+            for cb in range(CB):
+                nc.tensor.matmul(
+                    ps[j][:], weights[name][:, cb, block(h)], y_bf[r][:, cb, :],
+                    start=cb == 0, stop=cb == CB - 1,
+                )
+
+        def project_q(j):
+            project("q", q_ps, j)
+
+        def keep_q(j):
+            h = j % CB
+            q[j] = waiting.tile([P, T], BF16, name="q")
+            nc.scalar.activation(q[j][:], q_ps[j][:], FUNC.Identity, bias=bq_col[:, h : h + 1])
+
+        def project_k(j):
+            project("k", k_ps, j)
+
+        def keep_k(j):
+            k[j] = waiting.tile([P, T], BF16, name="k")
+            nc.scalar.copy(k[j][:], k_ps[j][:])
+
         def project_v(j):
             r, b = divmod(j, TB)
-            v_ps = product.tile([P, C], F32, name="v_ps", tag="product")
+            v_ps[j] = bank("v_ps")
             for cb in range(CB):
                 nc.tensor.matmul(
-                    v_ps[:], y_bf[r][:, cb, block(b)], weights["v"][:, cb, :],
+                    v_ps[j][:], y_bf[r][:, cb, block(b)], weights["v"][:, cb, :],
                     start=cb == 0, stop=cb == CB - 1,
                 )
+
+        def keep_v(j):
             v[j] = long_waiting.tile([P, C], BF16, name="v")
-            nc.scalar.copy(v[j][:], v_ps[:])
+            nc.scalar.copy(v[j][:], v_ps[j][:])
 
-        def project_qk(j):
+        def score_pair(g):
+            j, i = divmod(g, PARTS)
             r, b = divmod(j, CB)
-            q_ps = product.tile([P, T], F32, name="q_ps", tag="product")
-            for cb in range(CB):
-                nc.tensor.matmul(
-                    q_ps[:], weights["q"][:, cb, block(b)], y_bf[r][:, cb, :],
-                    start=cb == 0, stop=cb == CB - 1,
-                )
-            q[j] = waiting.tile([P, T], BF16, name="q")
-            nc.scalar.activation(q[j][:], q_ps[:], FUNC.Identity, bias=bq_col[:, b : b + 1])
-            k_ps = product.tile([P, T], F32, name="k_ps", tag="product")
-            for cb in range(CB):
-                nc.tensor.matmul(
-                    k_ps[:], weights["k"][:, cb, block(b)], y_bf[r][:, cb, :],
-                    start=cb == 0, stop=cb == CB - 1,
-                )
-            k[j] = waiting.tile([P, T], BF16, name="k")
-            nc.scalar.copy(k[j][:], k_ps[:])
+            h, tb = (i, b) if r == LAST else (b, i)
+            s_ps[g] = score.tile([P, T], F32, name="s_ps")
+            nc.tensor.matmul(
+                s_ps[g][:], q[r * CB + h][:, block(tb)], k[r * CB + h][:], start=True, stop=True
+            )
 
-        def attended(j):
+        def exponentials(g):
+            minus_s = ring.tile([P, T], F32, name="minus_s")
+            minus_max = ring.tile([P, 1], F32, name="minus_max")
+            nc.vector.tensor_scalar(
+                minus_s[:], s_ps[g][:], -SCORE_SCALE, None, ALU.mult, ALU.min,
+                accum_out=minus_max[:],
+            )
+            e[g] = ring.tile([P, T], F32, name="e")
+            e_sum[g] = ring.tile([P, 1], F32, name="e_sum")
+            nc.scalar.activation(
+                e[g][:], minus_s[:], FUNC.Exp, bias=minus_max[:], scale=-1.0,
+                accum_out=e_sum[g][:],
+            )
+
+        def probabilities(g):
+            one_over_sum = ring.tile([P, 1], F32, name="one_over_sum")
+            nc.vector.reciprocal(one_over_sum[:], e_sum[g][:])
+            p[g] = ring.tile([P, T], BF16, name="p")
+            nc.vector.tensor_scalar_mul(p[g][:], e[g][:], one_over_sum[:])
+
+        def flip_pair(g):
+            p_ps[g] = flip_p.tile([P, TB, P], BF16, name="p_ps")
+            for ub in range(TB):
+                nc.tensor.transpose(p_ps[g][:, ub, :], p[g][:, block(ub)], ident_bf16[:])
+
+        def keep_pair(g):
+            j, i = divmod(g, PARTS)
+            if i == 0:
+                p_flipped[j] = thrice.tile([P, TB, T], BF16, name="p_flipped")
+            nc.scalar.copy(p_flipped[j][:, :, block(i)], p_ps[g][:])
+
+        def heads_of(j):
             r, b = divmod(j, CB)
-            return [(h, b) for h in range(CB)] if r == LAST else [(b, tb) for tb in range(TB)]
+            return [(h, block(h)) for h in range(CB)] if r == LAST else [(b, slice(0, T))]
 
-        def probabilities(j):
-            p_flipped[j] = thrice.tile([P, TB, T], BF16, name="p_flipped")
-            for i, (h, tb) in enumerate(attended(j)):
-                head = j // CB * CB + h
-                s_ps = score.tile([P, T], F32, name="s_ps")
-                nc.tensor.matmul(
-                    s_ps[:], q[head][:, block(tb)], k[head][:], start=True, stop=True
-                )
-                minus_s = ring.tile([P, T], F32, name="minus_s")
-                minus_max = ring.tile([P, 1], F32, name="minus_max")
-                nc.vector.tensor_scalar(
-                    minus_s[:], s_ps[:], -SCORE_SCALE, None, ALU.mult, ALU.min,
-                    accum_out=minus_max[:],
-                )
-                e = ring.tile([P, T], F32, name="e")
-                e_sum = ring.tile([P, 1], F32, name="e_sum")
-                nc.scalar.activation(
-                    e[:], minus_s[:], FUNC.Exp, bias=minus_max[:], scale=-1.0, accum_out=e_sum[:]
-                )
-                one_over_sum = ring.tile([P, 1], F32, name="one_over_sum")
-                nc.vector.reciprocal(one_over_sum[:], e_sum[:])
-                p = ring.tile([P, T], BF16, name="p")
-                nc.vector.tensor_scalar_mul(p[:], e[:], one_over_sum[:])
-                p_ps = flip_p.tile([P, TB, P], BF16, name="p_ps")
-                for ub in range(TB):
-                    nc.tensor.transpose(p_ps[:, ub, :], p[:, block(ub)], ident_bf16[:])
-                nc.scalar.copy(p_flipped[j][:, :, block(i)], p_ps[:])
-
-        def context(j):
-            r, b = divmod(j, CB)
-            runs = [(h, block(h)) for h in range(CB)] if r == LAST else [(b, slice(0, T))]
-            ctx_ps = product.tile([P, T], F32, name="ctx_ps", tag="product")
-            ctx[j] = waiting.tile([P, T], BF16, name="ctx")
-            for h, columns in runs:
+        def make_ctx(j):
+            r = j // CB
+            ctx_ps[j] = bank("ctx_ps")
+            for h, columns in heads_of(j):
                 for ub in range(TB):
                     nc.tensor.matmul(
-                        ctx_ps[:, columns], v[r * TB + ub][:, block(h)], p_flipped[j][:, ub, columns],
-                        start=ub == 0, stop=ub == TB - 1,
+                        ctx_ps[j][:, columns], v[r * TB + ub][:, block(h)],
+                        p_flipped[j][:, ub, columns], start=ub == 0, stop=ub == TB - 1,
                     )
-            for h, columns in runs:
+
+        def keep_ctx(j):
+            ctx[j] = waiting.tile([P, T], BF16, name="ctx")
+            for h, columns in heads_of(j):
                 nc.scalar.activation(
-                    ctx[j][:, columns], ctx_ps[:, columns], FUNC.Identity, bias=bv_col[:, h : h + 1]
+                    ctx[j][:, columns], ctx_ps[j][:, columns], FUNC.Identity,
+                    bias=bv_col[:, h : h + 1],
+                )
+
+        def project_out(j):
+            r, tb = divmod(j, TB)
+            o_ps[j] = bank("o_ps")
+            for h in range(CB):
+                columns = ctx[j][:, block(h)] if r == LAST else ctx[r * CB + h][:, block(tb)]
+                nc.tensor.matmul(
+                    o_ps[j][:], columns, weights["o"][:, h, :], start=h == 0, stop=h == CB - 1
                 )
 
         def add_residual(j):
-            r, tb = divmod(j, TB)
-            o_ps = product.tile([P, C], F32, name="o_ps", tag="product")
-            for cb in range(CB):
-                nc.tensor.matmul(
-                    o_ps[:],
-                    ctx[j][:, block(cb)] if r == LAST else ctx[r * CB + cb][:, block(tb)],
-                    weights["o"][:, cb, :],
-                    start=cb == 0, stop=cb == CB - 1,
-                )
             z[j] = thrice.tile([P, C], F32, name="z")
-            nc.vector.tensor_tensor(z[j][:], o_ps[:], y_bo[j][:], ALU.add)
+            nc.vector.tensor_tensor(z[j][:], o_ps[j][:], y_bo[j][:], ALU.add)
+            moments_z[j] = moments(z[j])
 
         def standardise_z(j):
-            mean, rstd = moments(z[j])
+            mean, rstd = moments_z[j]
             z_hat[j] = thrice.tile([P, C], F32, name="z_hat")
             nc.vector.tensor_scalar(z_hat[j][:], z[j][:], mean, rstd, ALU.subtract, ALU.mult)
 
+        def flip_z(j):
+            out_ps[j] = bank("out_ps")
+            for cb in range(CB):
+                nc.tensor.transpose(out_ps[j][:, block(cb)], z_hat[j][:, block(cb)], ident_f32[:])
+
         def write_out(j):
-            back_ps = channels_first(z_hat[j], flip_x, "x_ps")
             out_sb = thrice.tile([P, CB, P], F32, name="out_sb")
             for cb in range(CB):
                 nc.scalar.activation(
-                    out_sb[:, cb, :], back_ps[:, cb, :], FUNC.Identity,
+                    out_sb[:, cb, :], out_ps[j][:, block(cb)], FUNC.Identity,
                     bias=shift1_col[:, cb : cb + 1], scale=gain1_col[:, cb : cb + 1],
                 )
             nc.sync.dma_start(out_blocks[:, :, block(j)], out_sb[:])
 
-        NEVER = STEPS * STEPS
+        def run(stage, j, count=STEPS):
+            if 0 <= j < count:
+                stage(j)
 
-        def qk_step(j):
-            return j - QK_LEAD if j < LAST * CB else NEVER
+        def z_blocks(step):
+            return [
+                j for j in range(STEPS)
+                if j + (LAST_RESIDUAL_LAG if j // CB == LAST else RESIDUAL_LAG) == step
+            ]
 
-        def last_qk_step(j):
-            return NEVER if j < LAST * CB else LAST * CB - LAST_QK_LEAD + j % CB // 2
+        def embed_part(j):
+            r, tb = divmod(j, TB)
+            return PARTS + tb if r == 1 else PARTS * (TB * r - TB - 1) + 3 * tb
 
-        def residual_step(j):
-            return j + (LAST_RESIDUAL_LAG if j // CB == LAST else RESIDUAL_LAG)
+        for cb in range(CB):
+            look_up(cb)
+        for j in range(TB):
+            flip_x(j)
+            keep_x(j)
+            measure_x(j)
+            normalise_x(j)
+        for j in range(TB):
+            flip_y(j)
+            keep_y(j)
+        project_q(0)
+        keep_q(0)
+        project_k(0)
+        keep_k(0)
 
-        for step in range(-EMBED_LEAD, STEPS + LAST_RESIDUAL_LAG + STORE_LAG):
-            stages = (
-                (probabilities, lambda j: j),
-                (add_residual, residual_step),
-                (embed, lambda j: j - EMBED_LEAD),
-                (standardise_z, lambda j: residual_step(j) + NORM_LAG),
-                (project_qk, qk_step),
-                (make_y, lambda j: j - Y_LEAD),
-                (project_v, lambda j: j - V_LEAD),
-                (write_out, lambda j: residual_step(j) + STORE_LAG),
-                (project_qk, last_qk_step),
-                (context, lambda j: j),
-            )
-            for stage, step_of in stages:
-                for j in range(STEPS):
-                    if step_of(j) == step:
-                        stage(j)
+        for step in range(STEPS + LAST_RESIDUAL_LAG + OUT_LAG + 1):
+            for part in range(PARTS):
+                pair = PARTS * step + part
+                run(score_pair, pair, PARTS * STEPS)
+                run(exponentials, pair - 1, PARTS * STEPS)
+                run(probabilities, pair - 2, PARTS * STEPS)
+                run(flip_pair, pair - 3, PARTS * STEPS)
+                run(keep_pair, pair - 4, PARTS * STEPS)
+                run(project_v, pair, TB)
+                run(keep_v, pair - 1, TB)
+                for j in range(TB, STEPS):
+                    if pair == embed_part(j - j % CB) - CB + j % CB:
+                        look_up(j)
+                    for lag, stage in (
+                        (0, flip_x), (1, keep_x), (2, measure_x), (3, normalise_x),
+                        (4, flip_y), (5, keep_y), (7, project_v), (8, keep_v),
+                    ):
+                        if pair == embed_part(j) + lag:
+                            stage(j)
+                if part == 0:
+                    for j in z_blocks(step - 1):
+                        add_residual(j)
+                if part == 1:
+                    for j in z_blocks(step - 1):
+                        standardise_z(j)
+                    run(make_ctx, step - CTX_LAG)
+                    if step + QK_LEAD <= LAST * CB:
+                        project_k(step + QK_LEAD)
+                if part == 2:
+                    run(keep_ctx, step - CTX_LAG)
+                    if step + QK_LEAD <= LAST * CB:
+                        keep_k(step + QK_LEAD)
+                    for j in z_blocks(step - OUT_LAG):
+                        flip_z(j)
+                    if step + QK_LEAD <= LAST * CB:
+                        project_q(step + QK_LEAD)
+                if part == 3:
+                    for j in z_blocks(step - OUT_LAG):
+                        write_out(j)
+                    if step + QK_LEAD <= LAST * CB:
+                        keep_q(step + QK_LEAD)
+                    for j in z_blocks(step):
+                        project_out(j)
+                h = pair - PARTS * LAST * CB + 2
+                if 0 < h < CB:
+                    project_q(LAST * CB + h)
+                    project_k(LAST * CB + h)
+                if 1 < h < CB + 1:
+                    keep_q(LAST * CB + h - 1)
+                    keep_k(LAST * CB + h - 1)

@@ -23,8 +23,8 @@ PARTS = CB
 LAST = SEQS - 1
 QK_LEAD = 1
 CTX_LAG = 2
-RESIDUAL_LAG = CTX_LAG + TB - 1
-LAST_RESIDUAL_LAG = CTX_LAG
+LAST_RESIDUAL_LAG = CTX_LAG + 1
+RESIDUAL_LAG = LAST_RESIDUAL_LAG + TB - 1
 OUT_LAG = 2
 
 FLOPS = 4 * 2 * C * C * N + 2 * 2 * SEQS * CB * T * T * P
@@ -45,7 +45,7 @@ def tile_ternaryberttiny_b_kernel(
         waiting = pools.enter_context(tc.tile_pool(name="waiting", bufs=2 * CB + 1))
         long_waiting = pools.enter_context(tc.tile_pool(name="long_waiting", bufs=3 * TB + 1))
         score = pools.enter_context(tc.psum_pool(name="score", bufs=2))
-        flip_p = pools.enter_context(tc.psum_pool(name="flip_p", bufs=2))
+        flip_e = pools.enter_context(tc.psum_pool(name="flip_e", bufs=2))
         product = pools.enter_context(tc.psum_pool(name="product", bufs=4))
 
         offsets = held.tile([P, N // 16], U16, name="offsets")
@@ -54,7 +54,9 @@ def tile_ternaryberttiny_b_kernel(
         pos_sb = [held.tile([P, T], F32, name=f"pos{cb}") for cb in range(CB)]
         for cb in range(CB):
             nc.sync.dma_start(tok_sb[cb][:], tok[block(cb), :])
-            nc.scalar.dma_start(pos_sb[cb][:], pos[block(cb), :])
+            nc.scalar.dma_start(pos_sb[cb][:, :P], pos[block(cb), :P])
+        for cb in range(CB):
+            nc.sync.dma_start(pos_sb[cb][:, P:], pos[block(cb), P:])
 
         def in_every_partition(vector, name):
             row = held.tile([P, C], F32, name=name)
@@ -70,12 +72,12 @@ def tile_ternaryberttiny_b_kernel(
         shift0_row = in_every_partition(shift0, "shift0_row")
         bo_row = in_every_partition(bo, "bo_row")
         bo_col = one_to_a_partition(bo, "bo_col")
-        bv_col = one_to_a_partition(bv, "bv_col")
         bq_col = one_to_a_partition(bq, "bq_col")
         weights = {}
         for name, w in (("v", wv), ("q", wq), ("k", wk), ("o", wo)):
             weights[name] = held.tile([P, CB, C], BF16, name=f"w{name}")
             nc.sync.dma_start(weights[name][:], w.rearrange("(cb p) m -> p cb m", p=P))
+        bv_row = in_every_partition(bv, "bv_row")
         gain1_col = one_to_a_partition(gain1, "gain1_col")
         shift1_col = one_to_a_partition(shift1, "shift1_col")
 
@@ -94,9 +96,10 @@ def tile_ternaryberttiny_b_kernel(
         out_blocks = out.rearrange("(cb p) j -> p cb j", p=P)
 
         x, y_bf = {}, {}
-        s_ps, e, e_sum, p, p_ps = {}, {}, {}, {}, {}
+        s_ps, minus_s, minus_max, e, e_ps = {}, {}, {}, {}, {}
         x_ps, y_ps, q_ps, k_ps, v_ps, ctx_ps, o_ps, out_ps = {}, {}, {}, {}, {}, {}, {}, {}
-        x_rows, moments_x, y_bo, q, k, v, p_flipped, ctx = {}, {}, {}, {}, {}, {}, {}, {}
+        centred, rstd, y_bo, q, k, v = {}, {}, {}, {}, {}, {}
+        sums, e_flipped, rows_ps, rows, ctx = {}, {}, {}, {}, {}
         z, moments_z, z_hat = {}, {}, {}
 
         def bank(name):
@@ -109,17 +112,17 @@ def tile_ternaryberttiny_b_kernel(
             nc.vector.bn_aggr(mean_var[:], stats[:])
             var_eps = ring.tile([P, 1], F32, name="var_eps")
             nc.vector.tensor_scalar_add(var_eps[:], mean_var[:, 1:2], EPS)
-            rstd = ring.tile([P, 1], F32, name="rstd")
-            nc.gpsimd.tensor_tensor(rstd[:], var_eps[:], minus_half[:], ALU.pow)
-            return mean_var[:, 0:1], rstd[:]
+            one_over_std = ring.tile([P, 1], F32, name="one_over_std")
+            nc.gpsimd.tensor_tensor(one_over_std[:], var_eps[:], minus_half[:], ALU.pow)
+            return mean_var[:, 0:1], one_over_std[:]
 
-        def look_up(j):
-            r, cb = divmod(j, CB)
-            if cb == 0:
+        def look_up(r, cb, tokens):
+            if r not in x:
                 x[r] = held.tile([P, CB, T], F32, name="x")
-            piece = offsets[:, r * (T // 16) : (r + 1) * (T // 16)]
+            start = (r * T + tokens.start) // 16
+            piece = offsets[:, start : start + (tokens.stop - tokens.start) // 16]
             nc.vector.tensor_tensor(
-                x[r][:, cb, :], tok_sb[cb][:].indirect(piece), pos_sb[cb][:], ALU.add
+                x[r][:, cb, tokens], tok_sb[cb][:].indirect(piece), pos_sb[cb][:, tokens], ALU.add
             )
 
         def flip_x(j):
@@ -128,22 +131,17 @@ def tile_ternaryberttiny_b_kernel(
             for cb in range(CB):
                 nc.tensor.transpose(x_ps[j][:, block(cb)], x[r][:, cb, block(tb)], ident_f32[:])
 
-        def keep_x(j):
-            x_rows[j] = ring.tile([P, C], F32, name="x_rows")
-            nc.scalar.copy(x_rows[j][:], x_ps[j][:])
-
-        def measure_x(j):
-            moments_x[j] = moments(x_rows[j])
+        def centre_x(j):
+            mean, rstd[j] = moments(x_ps[j])
+            centred[j] = ring.tile([P, C], F32, name="centred")
+            nc.vector.scalar_tensor_tensor(
+                centred[j][:], x_ps[j][:], mean, gain0_row[:], ALU.subtract, ALU.mult
+            )
 
         def normalise_x(j):
-            mean, rstd = moments_x[j]
-            centred = ring.tile([P, C], F32, name="centred")
-            nc.vector.scalar_tensor_tensor(
-                centred[:], x_rows[j][:], mean, gain0_row[:], ALU.subtract, ALU.mult
-            )
             y_bo[j] = held.tile([P, C], F32, name=f"y_bo{j}")
             nc.vector.scalar_tensor_tensor(
-                y_bo[j][:], centred[:], rstd, shift0_bo_row[:], ALU.mult, ALU.add
+                y_bo[j][:], centred[j][:], rstd[j], shift0_bo_row[:], ALU.mult, ALU.add
             )
 
         def flip_y(j):
@@ -207,64 +205,73 @@ def tile_ternaryberttiny_b_kernel(
                 s_ps[g][:], q[r * CB + h][:, block(tb)], k[r * CB + h][:], start=True, stop=True
             )
 
-        def exponentials(g):
-            minus_s = ring.tile([P, T], F32, name="minus_s")
-            minus_max = ring.tile([P, 1], F32, name="minus_max")
+        def keep_scores(g):
+            minus_s[g] = ring.tile([P, T], F32, name="minus_s")
+            minus_max[g] = ring.tile([P, 1], F32, name="minus_max")
             nc.vector.tensor_scalar(
-                minus_s[:], s_ps[g][:], -SCORE_SCALE, None, ALU.mult, ALU.min,
-                accum_out=minus_max[:],
-            )
-            e[g] = ring.tile([P, T], F32, name="e")
-            e_sum[g] = ring.tile([P, 1], F32, name="e_sum")
-            nc.scalar.activation(
-                e[g][:], minus_s[:], FUNC.Exp, bias=minus_max[:], scale=-1.0,
-                accum_out=e_sum[g][:],
+                minus_s[g][:], s_ps[g][:], -SCORE_SCALE, None, ALU.mult, ALU.min,
+                accum_out=minus_max[g][:],
             )
 
-        def probabilities(g):
-            one_over_sum = ring.tile([P, 1], F32, name="one_over_sum")
-            nc.vector.reciprocal(one_over_sum[:], e_sum[g][:])
-            p[g] = ring.tile([P, T], BF16, name="p")
-            nc.vector.tensor_scalar_mul(p[g][:], e[g][:], one_over_sum[:])
+        def exponentials(g):
+            j, i = divmod(g, PARTS)
+            if i == 0:
+                sums[j] = thrice.tile([P, PARTS], F32, name="sums")
+            e[g] = ring.tile([P, T], BF16, name="e")
+            nc.scalar.activation(
+                e[g][:], minus_s[g][:], FUNC.Exp, bias=minus_max[g][:], scale=-1.0,
+                accum_out=sums[j][:, i : i + 1],
+            )
 
         def flip_pair(g):
-            p_ps[g] = flip_p.tile([P, TB, P], BF16, name="p_ps")
+            e_ps[g] = flip_e.tile([P, TB, P], BF16, name="e_ps")
             for ub in range(TB):
-                nc.tensor.transpose(p_ps[g][:, ub, :], p[g][:, block(ub)], ident_bf16[:])
+                nc.tensor.transpose(e_ps[g][:, ub, :], e[g][:, block(ub)], ident_bf16[:])
 
         def keep_pair(g):
             j, i = divmod(g, PARTS)
             if i == 0:
-                p_flipped[j] = thrice.tile([P, TB, T], BF16, name="p_flipped")
-            nc.scalar.copy(p_flipped[j][:, :, block(i)], p_ps[g][:])
+                e_flipped[j] = thrice.tile([P, TB, T], BF16, name="e_flipped")
+            nc.scalar.copy(e_flipped[j][:, :, block(i)], e_ps[g][:])
 
-        def heads_of(j):
+        def head_of(j, i):
             r, b = divmod(j, CB)
-            return [(h, block(h)) for h in range(CB)] if r == LAST else [(b, slice(0, T))]
+            return i if r == LAST else b
 
         def make_ctx(j):
             r = j // CB
-            ctx_ps[j] = bank("ctx_ps")
-            for h, columns in heads_of(j):
+            rows_ps[j] = bank("rows_ps")
+            for i in range(PARTS):
                 for ub in range(TB):
                     nc.tensor.matmul(
-                        ctx_ps[j][:, columns], v[r * TB + ub][:, block(h)],
-                        p_flipped[j][:, ub, columns], start=ub == 0, stop=ub == TB - 1,
+                        rows_ps[j][:, block(i)], e_flipped[j][:, ub, block(i)],
+                        v[r * TB + ub][:, block(head_of(j, i))], start=ub == 0, stop=ub == TB - 1,
                     )
 
-        def keep_ctx(j):
-            ctx[j] = waiting.tile([P, T], BF16, name="ctx")
-            for h, columns in heads_of(j):
-                nc.scalar.activation(
-                    ctx[j][:, columns], ctx_ps[j][:, columns], FUNC.Identity,
-                    bias=bv_col[:, h : h + 1],
+        def divide_ctx(j):
+            one_over_sum = ring.tile([P, PARTS], F32, name="one_over_sum")
+            nc.vector.reciprocal(one_over_sum[:], sums[j][:])
+            rows[j] = thrice.tile([P, T], BF16, name="rows")
+            for i in range(PARTS):
+                nc.vector.scalar_tensor_tensor(
+                    rows[j][:, block(i)], rows_ps[j][:, block(i)], one_over_sum[:, i : i + 1],
+                    bv_row[:, block(head_of(j, i))], ALU.mult, ALU.add,
                 )
+
+        def flip_ctx(j):
+            ctx_ps[j] = product.tile([P, PARTS, P], BF16, name="ctx_ps", tag="product")
+            for i in range(PARTS):
+                nc.tensor.transpose(ctx_ps[j][:, i, :], rows[j][:, block(i)], ident_bf16[:])
+
+        def keep_ctx(j):
+            ctx[j] = waiting.tile([P, PARTS, P], BF16, name="ctx")
+            nc.vector.tensor_copy(ctx[j][:], ctx_ps[j][:])
 
         def project_out(j):
             r, tb = divmod(j, TB)
             o_ps[j] = bank("o_ps")
             for h in range(CB):
-                columns = ctx[j][:, block(h)] if r == LAST else ctx[r * CB + h][:, block(tb)]
+                columns = ctx[j][:, h, :] if r == LAST else ctx[r * CB + h][:, tb, :]
                 nc.tensor.matmul(
                     o_ps[j][:], columns, weights["o"][:, h, :], start=h == 0, stop=h == CB - 1
                 )
@@ -275,9 +282,11 @@ def tile_ternaryberttiny_b_kernel(
             moments_z[j] = moments(z[j])
 
         def standardise_z(j):
-            mean, rstd = moments_z[j]
+            mean, one_over_std = moments_z[j]
             z_hat[j] = thrice.tile([P, C], F32, name="z_hat")
-            nc.vector.tensor_scalar(z_hat[j][:], z[j][:], mean, rstd, ALU.subtract, ALU.mult)
+            nc.vector.tensor_scalar(
+                z_hat[j][:], z[j][:], mean, one_over_std, ALU.subtract, ALU.mult
+            )
 
         def flip_z(j):
             out_ps[j] = bank("out_ps")
@@ -307,63 +316,74 @@ def tile_ternaryberttiny_b_kernel(
             r, tb = divmod(j, TB)
             return PARTS + tb if r == 1 else PARTS * (TB * r - TB - 1) + 3 * tb
 
-        for cb in range(CB):
-            look_up(cb)
-        for j in range(TB):
+        def begin(j):
+            for cb in range(CB):
+                look_up(0, cb, block(j))
             flip_x(j)
-            keep_x(j)
-            measure_x(j)
+            centre_x(j)
             normalise_x(j)
+
+        begin(0)
+        begin(1)
         for j in range(TB):
             flip_y(j)
             keep_y(j)
+            if j + 2 < TB:
+                begin(j + 2)
+            if j < TB - 1:
+                project_v(j)
+                keep_v(j)
         project_q(0)
         keep_q(0)
         project_k(0)
         keep_k(0)
+        project_v(TB - 1)
+        keep_v(TB - 1)
 
         for step in range(STEPS + LAST_RESIDUAL_LAG + OUT_LAG + 1):
             for part in range(PARTS):
                 pair = PARTS * step + part
                 run(score_pair, pair, PARTS * STEPS)
-                run(exponentials, pair - 1, PARTS * STEPS)
-                run(probabilities, pair - 2, PARTS * STEPS)
+                run(keep_scores, pair - 1, PARTS * STEPS)
+                run(exponentials, pair - 2, PARTS * STEPS)
                 run(flip_pair, pair - 3, PARTS * STEPS)
                 run(keep_pair, pair - 4, PARTS * STEPS)
-                run(project_v, pair, TB)
-                run(keep_v, pair - 1, TB)
                 for j in range(TB, STEPS):
-                    if pair == embed_part(j - j % CB) - CB + j % CB:
-                        look_up(j)
+                    if j < 2 * TB and pair == embed_part(j) - 1:
+                        for cb in range(CB):
+                            look_up(1, cb, block(j - TB))
+                    if j >= 2 * TB and pair == embed_part(j - j % CB) - CB + j % CB:
+                        look_up(j // CB, j % CB, slice(0, T))
                     for lag, stage in (
-                        (0, flip_x), (1, keep_x), (2, measure_x), (3, normalise_x),
-                        (4, flip_y), (5, keep_y), (7, project_v), (8, keep_v),
+                        (0, flip_x), (1, centre_x), (2, normalise_x),
+                        (3, flip_y), (4, keep_y), (6, project_v), (7, keep_v),
                     ):
                         if pair == embed_part(j) + lag:
                             stage(j)
                 if part == 0:
-                    for j in z_blocks(step - 1):
+                    for j in z_blocks(step):
                         add_residual(j)
-                if part == 1:
-                    for j in z_blocks(step - 1):
-                        standardise_z(j)
                     run(make_ctx, step - CTX_LAG)
-                    if step + QK_LEAD <= LAST * CB:
-                        project_k(step + QK_LEAD)
-                if part == 2:
-                    run(keep_ctx, step - CTX_LAG)
-                    if step + QK_LEAD <= LAST * CB:
-                        keep_k(step + QK_LEAD)
+                if part == 1:
+                    run(divide_ctx, step - CTX_LAG)
                     for j in z_blocks(step - OUT_LAG):
                         flip_z(j)
                     if step + QK_LEAD <= LAST * CB:
-                        project_q(step + QK_LEAD)
-                if part == 3:
+                        project_k(step + QK_LEAD)
+                if part == 2:
+                    for j in z_blocks(step):
+                        standardise_z(j)
                     for j in z_blocks(step - OUT_LAG):
                         write_out(j)
                     if step + QK_LEAD <= LAST * CB:
+                        keep_k(step + QK_LEAD)
+                        project_q(step + QK_LEAD)
+                    run(flip_ctx, step - CTX_LAG)
+                if part == 3:
+                    run(keep_ctx, step - CTX_LAG)
+                    if step + QK_LEAD <= LAST * CB:
                         keep_q(step + QK_LEAD)
-                    for j in z_blocks(step):
+                    for j in z_blocks(step + 1):
                         project_out(j)
                 h = pair - PARTS * LAST * CB + 2
                 if 0 < h < CB:

from contextlib import ExitStack

import concourse.mybir as mybir
from concourse.masks import make_identity

F32, BF16, U16 = mybir.dt.float32, mybir.dt.bfloat16, mybir.dt.uint16
ALU = mybir.AluOpType
FUNC = mybir.ActivationFunctionType

P = 128
C = 512
WORDS = 1024
T = 512
SEQS = 4
N = SEQS * T
CB = C // P
TB = T // P
EPS = 1e-5
SCORE_SCALE = P**-0.5

STEPS = SEQS * CB
PARTS = CB
LAST = SEQS - 1
QK_LEAD = 1
CTX_LAG = 2
LAST_RESIDUAL_LAG = CTX_LAG + 1
RESIDUAL_LAG = LAST_RESIDUAL_LAG + TB - 1
OUT_LAG = 2

FLOPS = 4 * 2 * C * C * N + 2 * 2 * SEQS * CB * T * T * P


def block(i):
    return slice(i * P, (i + 1) * P)


def tile_ternaryberttiny_b_kernel(
    tc, tok, pos, gain0, shift0, wq, bq, wk, wv, bv, wo, bo, gain1, shift1, offs, out
):
    nc = tc.nc
    with ExitStack() as pools:
        held = pools.enter_context(tc.tile_pool(name="held", bufs=1))
        thrice = pools.enter_context(tc.tile_pool(name="thrice", bufs=3))
        ring = pools.enter_context(tc.tile_pool(name="ring", bufs=4))
        waiting = pools.enter_context(tc.tile_pool(name="waiting", bufs=2 * CB + 1))
        long_waiting = pools.enter_context(tc.tile_pool(name="long_waiting", bufs=3 * TB + 1))
        score = pools.enter_context(tc.psum_pool(name="score", bufs=2))
        flip_e = pools.enter_context(tc.psum_pool(name="flip_e", bufs=2))
        product = pools.enter_context(tc.psum_pool(name="product", bufs=4))

        offsets = held.tile([P, N // 16], U16, name="offsets")
        nc.sync.dma_start(offsets[:], offs)
        tok_sb = [held.tile([P, WORDS], F32, name=f"tok{cb}") for cb in range(CB)]
        pos_sb = [held.tile([P, T], F32, name=f"pos{cb}") for cb in range(CB)]
        for cb in range(CB):
            nc.sync.dma_start(tok_sb[cb][:], tok[block(cb), :])
            nc.scalar.dma_start(pos_sb[cb][:, :P], pos[block(cb), :P])
        for cb in range(CB):
            nc.sync.dma_start(pos_sb[cb][:, P:], pos[block(cb), P:])

        def in_every_partition(vector, name):
            row = held.tile([P, C], F32, name=name)
            nc.sync.dma_start(row[:], vector.rearrange("c one -> (c one)").partition_broadcast(P))
            return row

        def one_to_a_partition(vector, name):
            column = held.tile([P, CB], F32, name=name)
            nc.scalar.dma_start(column[:], vector.rearrange("(cb p) one -> p (cb one)", p=P))
            return column

        gain0_row = in_every_partition(gain0, "gain0_row")
        shift0_row = in_every_partition(shift0, "shift0_row")
        bo_row = in_every_partition(bo, "bo_row")
        bo_col = one_to_a_partition(bo, "bo_col")
        bq_col = one_to_a_partition(bq, "bq_col")
        weights = {}
        for name, w in (("v", wv), ("q", wq), ("k", wk), ("o", wo)):
            weights[name] = held.tile([P, CB, C], BF16, name=f"w{name}")
            nc.sync.dma_start(weights[name][:], w.rearrange("(cb p) m -> p cb m", p=P))
        bv_row = in_every_partition(bv, "bv_row")
        gain1_col = one_to_a_partition(gain1, "gain1_col")
        shift1_col = one_to_a_partition(shift1, "shift1_col")

        shift0_bo_row = held.tile([P, C], F32, name="shift0_bo_row")
        nc.gpsimd.tensor_tensor(shift0_bo_row[:], shift0_row[:], bo_row[:], ALU.add)
        minus_bo_col = held.tile([P, CB], F32, name="minus_bo_col")
        nc.gpsimd.tensor_scalar_mul(minus_bo_col[:], bo_col[:], -1.0)

        ident_f32 = held.tile([P, P], F32, name="ident_f32")
        make_identity(nc, ident_f32[:])
        ident_bf16 = held.tile([P, P], BF16, name="ident_bf16")
        make_identity(nc, ident_bf16[:])
        minus_half = held.tile([P, 1], F32, name="minus_half")
        nc.vector.memset(minus_half[:], -0.5)

        out_blocks = out.rearrange("(cb p) j -> p cb j", p=P)

        x, y_bf = {}, {}
        s_ps, minus_s, minus_max, e, e_ps = {}, {}, {}, {}, {}
        x_ps, y_ps, q_ps, k_ps, v_ps, ctx_ps, o_ps, out_ps = {}, {}, {}, {}, {}, {}, {}, {}
        centred, rstd, y_bo, q, k, v = {}, {}, {}, {}, {}, {}
        sums, e_flipped, rows_ps, rows, ctx = {}, {}, {}, {}, {}
        z, moments_z, z_hat = {}, {}, {}

        def bank(name):
            return product.tile([P, T], F32, name=name, tag="product")

        def moments(a):
            stats = ring.tile([P, 6], F32, name="stats")
            nc.vector.bn_stats(stats[:], a[:])
            mean_var = ring.tile([P, 2], F32, name="mean_var")
            nc.vector.bn_aggr(mean_var[:], stats[:])
            var_eps = ring.tile([P, 1], F32, name="var_eps")
            nc.vector.tensor_scalar_add(var_eps[:], mean_var[:, 1:2], EPS)
            one_over_std = ring.tile([P, 1], F32, name="one_over_std")
            nc.gpsimd.tensor_tensor(one_over_std[:], var_eps[:], minus_half[:], ALU.pow)
            return mean_var[:, 0:1], one_over_std[:]

        def look_up(r, cb, tokens):
            if r not in x:
                x[r] = held.tile([P, CB, T], F32, name="x")
            start = (r * T + tokens.start) // 16
            piece = offsets[:, start : start + (tokens.stop - tokens.start) // 16]
            nc.vector.tensor_tensor(
                x[r][:, cb, tokens], tok_sb[cb][:].indirect(piece), pos_sb[cb][:, tokens], ALU.add
            )

        def flip_x(j):
            r, tb = divmod(j, TB)
            x_ps[j] = bank("x_ps")
            for cb in range(CB):
                nc.tensor.transpose(x_ps[j][:, block(cb)], x[r][:, cb, block(tb)], ident_f32[:])

        def centre_x(j):
            mean, rstd[j] = moments(x_ps[j])
            centred[j] = ring.tile([P, C], F32, name="centred")
            nc.vector.scalar_tensor_tensor(
                centred[j][:], x_ps[j][:], mean, gain0_row[:], ALU.subtract, ALU.mult
            )

        def normalise_x(j):
            y_bo[j] = held.tile([P, C], F32, name=f"y_bo{j}")
            nc.vector.scalar_tensor_tensor(
                y_bo[j][:], centred[j][:], rstd[j], shift0_bo_row[:], ALU.mult, ALU.add
            )

        def flip_y(j):
            y_ps[j] = bank("y_ps")
            for cb in range(CB):
                nc.tensor.transpose(y_ps[j][:, block(cb)], y_bo[j][:, block(cb)], ident_f32[:])

        def keep_y(j):
            r, tb = divmod(j, TB)
            if tb == 0:
                y_bf[r] = thrice.tile([P, CB, T], BF16, name="y_bf")
            for cb in range(CB):
                nc.scalar.activation(
                    y_bf[r][:, cb, block(tb)], y_ps[j][:, block(cb)], FUNC.Identity,
                    bias=minus_bo_col[:, cb : cb + 1],
                )

        def project(name, ps, j):
            r, h = divmod(j, CB)
            ps[j] = bank(f"{name}_ps")
            for cb in range(CB):
                nc.tensor.matmul(
                    ps[j][:], weights[name][:, cb, block(h)], y_bf[r][:, cb, :],
                    start=cb == 0, stop=cb == CB - 1,
                )

        def project_q(j):
            project("q", q_ps, j)

        def keep_q(j):
            h = j % CB
            q[j] = waiting.tile([P, T], BF16, name="q")
            nc.scalar.activation(q[j][:], q_ps[j][:], FUNC.Identity, bias=bq_col[:, h : h + 1])

        def project_k(j):
            project("k", k_ps, j)

        def keep_k(j):
            k[j] = waiting.tile([P, T], BF16, name="k")
            nc.scalar.copy(k[j][:], k_ps[j][:])

        def project_v(j):
            r, b = divmod(j, TB)
            v_ps[j] = bank("v_ps")
            for cb in range(CB):
                nc.tensor.matmul(
                    v_ps[j][:], y_bf[r][:, cb, block(b)], weights["v"][:, cb, :],
                    start=cb == 0, stop=cb == CB - 1,
                )

        def keep_v(j):
            v[j] = long_waiting.tile([P, C], BF16, name="v")
            nc.scalar.copy(v[j][:], v_ps[j][:])

        def score_pair(g):
            j, i = divmod(g, PARTS)
            r, b = divmod(j, CB)
            h, tb = (i, b) if r == LAST else (b, i)
            s_ps[g] = score.tile([P, T], F32, name="s_ps")
            nc.tensor.matmul(
                s_ps[g][:], q[r * CB + h][:, block(tb)], k[r * CB + h][:], start=True, stop=True
            )

        def keep_scores(g):
            minus_s[g] = ring.tile([P, T], F32, name="minus_s")
            minus_max[g] = ring.tile([P, 1], F32, name="minus_max")
            nc.vector.tensor_scalar(
                minus_s[g][:], s_ps[g][:], -SCORE_SCALE, None, ALU.mult, ALU.min,
                accum_out=minus_max[g][:],
            )

        def exponentials(g):
            j, i = divmod(g, PARTS)
            if i == 0:
                sums[j] = thrice.tile([P, PARTS], F32, name="sums")
            e[g] = ring.tile([P, T], BF16, name="e")
            nc.scalar.activation(
                e[g][:], minus_s[g][:], FUNC.Exp, bias=minus_max[g][:], scale=-1.0,
                accum_out=sums[j][:, i : i + 1],
            )

        def flip_pair(g):
            e_ps[g] = flip_e.tile([P, TB, P], BF16, name="e_ps")
            for ub in range(TB):
                nc.tensor.transpose(e_ps[g][:, ub, :], e[g][:, block(ub)], ident_bf16[:])

        def keep_pair(g):
            j, i = divmod(g, PARTS)
            if i == 0:
                e_flipped[j] = thrice.tile([P, TB, T], BF16, name="e_flipped")
            nc.scalar.copy(e_flipped[j][:, :, block(i)], e_ps[g][:])

        def head_of(j, i):
            r, b = divmod(j, CB)
            return i if r == LAST else b

        def make_ctx(j):
            r = j // CB
            rows_ps[j] = bank("rows_ps")
            for i in range(PARTS):
                for ub in range(TB):
                    nc.tensor.matmul(
                        rows_ps[j][:, block(i)], e_flipped[j][:, ub, block(i)],
                        v[r * TB + ub][:, block(head_of(j, i))], start=ub == 0, stop=ub == TB - 1,
                    )

        def divide_ctx(j):
            one_over_sum = ring.tile([P, PARTS], F32, name="one_over_sum")
            nc.vector.reciprocal(one_over_sum[:], sums[j][:])
            rows[j] = thrice.tile([P, T], BF16, name="rows")
            for i in range(PARTS):
                nc.vector.scalar_tensor_tensor(
                    rows[j][:, block(i)], rows_ps[j][:, block(i)], one_over_sum[:, i : i + 1],
                    bv_row[:, block(head_of(j, i))], ALU.mult, ALU.add,
                )

        def flip_ctx(j):
            ctx_ps[j] = product.tile([P, PARTS, P], BF16, name="ctx_ps", tag="product")
            for i in range(PARTS):
                nc.tensor.transpose(ctx_ps[j][:, i, :], rows[j][:, block(i)], ident_bf16[:])

        def keep_ctx(j):
            ctx[j] = waiting.tile([P, PARTS, P], BF16, name="ctx")
            nc.vector.tensor_copy(ctx[j][:], ctx_ps[j][:])

        def project_out(j):
            r, tb = divmod(j, TB)
            o_ps[j] = bank("o_ps")
            for h in range(CB):
                columns = ctx[j][:, h, :] if r == LAST else ctx[r * CB + h][:, tb, :]
                nc.tensor.matmul(
                    o_ps[j][:], columns, weights["o"][:, h, :], start=h == 0, stop=h == CB - 1
                )

        def add_residual(j):
            z[j] = thrice.tile([P, C], F32, name="z")
            nc.vector.tensor_tensor(z[j][:], o_ps[j][:], y_bo[j][:], ALU.add)
            moments_z[j] = moments(z[j])

        def standardise_z(j):
            mean, one_over_std = moments_z[j]
            z_hat[j] = thrice.tile([P, C], F32, name="z_hat")
            nc.vector.tensor_scalar(
                z_hat[j][:], z[j][:], mean, one_over_std, ALU.subtract, ALU.mult
            )

        def flip_z(j):
            out_ps[j] = bank("out_ps")
            for cb in range(CB):
                nc.tensor.transpose(out_ps[j][:, block(cb)], z_hat[j][:, block(cb)], ident_f32[:])

        def write_out(j):
            out_sb = thrice.tile([P, CB, P], F32, name="out_sb")
            for cb in range(CB):
                nc.scalar.activation(
                    out_sb[:, cb, :], out_ps[j][:, block(cb)], FUNC.Identity,
                    bias=shift1_col[:, cb : cb + 1], scale=gain1_col[:, cb : cb + 1],
                )
            nc.sync.dma_start(out_blocks[:, :, block(j)], out_sb[:])

        def run(stage, j, count=STEPS):
            if 0 <= j < count:
                stage(j)

        def z_blocks(step):
            return [
                j for j in range(STEPS)
                if j + (LAST_RESIDUAL_LAG if j // CB == LAST else RESIDUAL_LAG) == step
            ]

        def embed_part(j):
            r, tb = divmod(j, TB)
            return PARTS + tb if r == 1 else PARTS * (TB * r - TB - 1) + 3 * tb

        def begin(j):
            for cb in range(CB):
                look_up(0, cb, block(j))
            flip_x(j)
            centre_x(j)
            normalise_x(j)

        begin(0)
        begin(1)
        for j in range(TB):
            flip_y(j)
            keep_y(j)
            if j + 2 < TB:
                begin(j + 2)
            if j < TB - 1:
                project_v(j)
                keep_v(j)
        project_q(0)
        keep_q(0)
        project_k(0)
        keep_k(0)
        project_v(TB - 1)
        keep_v(TB - 1)

        for step in range(STEPS + LAST_RESIDUAL_LAG + OUT_LAG + 1):
            for part in range(PARTS):
                pair = PARTS * step + part
                run(score_pair, pair, PARTS * STEPS)
                run(keep_scores, pair - 1, PARTS * STEPS)
                run(exponentials, pair - 2, PARTS * STEPS)
                run(flip_pair, pair - 3, PARTS * STEPS)
                run(keep_pair, pair - 4, PARTS * STEPS)
                for j in range(TB, STEPS):
                    if j < 2 * TB and pair == embed_part(j) - 1:
                        for cb in range(CB):
                            look_up(1, cb, block(j - TB))
                    if j >= 2 * TB and pair == embed_part(j - j % CB) - CB + j % CB:
                        look_up(j // CB, j % CB, slice(0, T))
                    for lag, stage in (
                        (0, flip_x), (1, centre_x), (2, normalise_x),
                        (3, flip_y), (4, keep_y), (6, project_v), (7, keep_v),
                    ):
                        if pair == embed_part(j) + lag:
                            stage(j)
                if part == 0:
                    for j in z_blocks(step):
                        add_residual(j)
                    run(make_ctx, step - CTX_LAG)
                if part == 1:
                    run(divide_ctx, step - CTX_LAG)
                    for j in z_blocks(step - OUT_LAG):
                        flip_z(j)
                    if step + QK_LEAD <= LAST * CB:
                        project_k(step + QK_LEAD)
                if part == 2:
                    for j in z_blocks(step):
                        standardise_z(j)
                    for j in z_blocks(step - OUT_LAG):
                        write_out(j)
                    if step + QK_LEAD <= LAST * CB:
                        keep_k(step + QK_LEAD)
                        project_q(step + QK_LEAD)
                    run(flip_ctx, step - CTX_LAG)
                if part == 3:
                    run(keep_ctx, step - CTX_LAG)
                    if step + QK_LEAD <= LAST * CB:
                        keep_q(step + QK_LEAD)
                    for j in z_blocks(step + 1):
                        project_out(j)
                h = pair - PARTS * LAST * CB + 2
                if 0 < h < CB:
                    project_q(LAST * CB + h)
                    project_k(LAST * CB + h)
                if 1 < h < CB + 1:
                    keep_q(LAST * CB + h - 1)
                    keep_k(LAST * CB + h - 1)
